import numpy as np
import ml_dtypes


def mxq(x, axis, fmt="e4m3"):
    dtype, down = {"e4m3": (ml_dtypes.float8_e4m3fn, 7), "e5m2": (ml_dtypes.float8_e5m2, 14)}[fmt]
    v = np.moveaxis(np.asarray(x, np.float32).astype(ml_dtypes.bfloat16).astype(np.float64), axis, -1)
    blocks = v.reshape(v.shape[:-1] + (-1, 32))
    amax = np.abs(blocks).max(-1, keepdims=True)
    byte = np.maximum(np.where(amax > 0, np.frexp(amax)[1] - 1 + 127, 0) - down, 1)
    scale = np.exp2(byte - 127.0)
    codes = (blocks / scale).astype(np.float32).astype(dtype).astype(np.float64)
    return np.moveaxis((codes * scale).reshape(v.shape), -1, axis)


WIDE = False


def mx_kscale(k):
    if not WIDE:
        return np.ones(k)
    levels = np.array([10, -10, 5, -5, 0])
    a = np.random.permutation(np.resize(levels, k // 512 * 4)).reshape(k // 512, 4)
    idx = np.arange(k)
    return np.exp2(a[idx // 512, idx % 128 // 32])


BF16 = ml_dtypes.bfloat16


def bf(x):
    return np.asarray(x, np.float32).astype(BF16)


def f64(x):
    return np.asarray(x).astype(np.float64)


B, S, E, H, G, D, C = 4, 1024, 1024, 4, 2, 128, 512
PER = H // G


def setup_inputs():
    s = mx_kscale(E)
    return {"q": bf(np.random.standard_normal((B, H, S, D)) * 1.4),
            "kg": bf(np.random.standard_normal((B, G, S, D)) * 1.4),
            "x": bf(np.random.standard_normal((B, S, E)) * s),
            "Wv": bf(np.random.standard_normal((G, E, D)) / np.sqrt(E) / s[None, :, None]),
            "bv": bf(np.random.standard_normal((G, D)) * 0.3)}


def reference(q, kg, x, Wv, bv):
    vg = (mxq(f64(x), 2, "e4m3")[:, None] @ mxq(f64(Wv), 1, "e4m3")[None]) + f64(bv)[None, :, None, :]
    vq = mxq(vg, 2, "e4m3")[:, :, None]
    qh = f64(q).reshape(B, G, PER, S, D)
    kt = f64(kg).transpose(0, 1, 3, 2)[:, :, None]
    rows = []
    for r in range(0, S, C):
        n = r + C
        sc = qh[:, :, :, r:n] @ kt[..., :n] * (1.0 / np.sqrt(D))
        masked = np.arange(n)[None, :] > np.arange(r, n)[:, None]
        sc = np.where(masked, -np.inf, sc)
        e = np.exp(sc - sc.max(-1, keepdims=True))
        rows.append((mxq(e, 4, "e4m3") @ vq[:, :, :, :n]) / e.sum(-1, keepdims=True))
    out = np.concatenate(rows, axis=3).reshape(B, H, S, D)
    return out.transpose(0, 2, 1, 3).reshape(B, S, H * D)

@@ -1,0 +1,397 @@
+import math
+from contextlib import ExitStack
+
+import concourse.mybir as mybir
+from concourse.masks import make_identity
+
+F32 = mybir.dt.float32
+BF16 = mybir.dt.bfloat16
+U32 = mybir.dt.uint32
+U8 = mybir.dt.uint8
+FP8X4 = mybir.dt.float8_e4m3fn_x4
+ALU = mybir.AluOpType
+ACT = mybir.ActivationFunctionType
+AX = mybir.AxisListType
+
+B, S, E, H, G, D = 4, 1024, 1024, 4, 2, 128
+P = 128
+PACK = 4
+K_PASS = P * PACK
+Q_TILES = S // P
+TILES_PER_PASS = K_PASS // P
+E_PASSES = E // K_PASS
+KEY_PASSES = S // K_PASS
+HEADS_PER_GROUP = H // G
+SCALE = 1.0 / math.sqrt(D)
+MASKED = -(2.0**100)
+
+FLOPS = 2 * B * G * S * E * D + 2 * 2 * B * H * D * (K_PASS * K_PASS + K_PASS * S)
+
+
+def tile_multiheadattention_pa_t_kernel(tc, q, kg, x, Wv, bv, out):
+    nc = tc.nc
+    with ExitStack() as ctx:
+        consts = ctx.enter_context(tc.tile_pool(name="consts", bufs=1))
+        batch = ctx.enter_context(tc.tile_pool(name="batch", bufs=2))
+        work = ctx.enter_context(tc.tile_pool(name="work", bufs=3))
+        ring = ctx.enter_context(tc.tile_pool(name="ring", bufs=4))
+        small = ctx.enter_context(tc.tile_pool(name="small", bufs=6))
+        psum_s = ctx.enter_context(tc.psum_pool(name="psum_s", bufs=4))
+        psum_t = ctx.enter_context(tc.psum_pool(name="psum_t", bufs=2))
+        psum_o = ctx.enter_context(tc.psum_pool(name="psum_o", bufs=2))
+        ctx.enter_context(tc.manual_schedule())
+
+        ident_f = consts.tile([P, P], F32, name="ident_f")
+        make_identity(nc, ident_f[:])
+        ident_bf = consts.tile([P, P], BF16, name="ident_bf")
+        make_identity(nc, ident_bf[:])
+        mask_f = consts.tile([P, P], F32, name="mask_f")
+        nc.gpsimd.memset(mask_f[:], 0.0)
+        nc.gpsimd.affine_select(
+            out=mask_f[:],
+            in_=mask_f[:],
+            pattern=[[-1, P]],
+            compare_op=ALU.is_ge,
+            fill=MASKED,
+            base=0,
+            channel_multiplier=1,
+        )
+        mask_bf = consts.tile([P, P], BF16, name="mask_bf")
+        nc.vector.tensor_copy(out=mask_bf[:], in_=mask_f[:])
+
+        e_diag = consts.tile([P, TILES_PER_PASS * H * K_PASS], BF16, name="e_diag")
+        e_diag_view = e_diag[:].rearrange("p (r h k) -> p r h k", r=TILES_PER_PASS, h=H)
+        for r in range(TILES_PER_PASS - 1):
+            nc.vector.memset(e_diag_view[:, r, :, (r + 1) * P :], 0.0)
+
+        def load_batch(b):
+            t = {}
+            t["x"] = batch.tile([P, (S // P) * E], BF16, name="x_sb")
+            rows = 2 * P
+            for a in range(S // rows):
+                nc.sync.dma_start(
+                    out=t["x"][:, a * 2 * E : (a + 1) * 2 * E],
+                    in_=x[b, a * rows : (a + 1) * rows, :].rearrange("(p e) k -> p (e k)", e=2),
+                )
+            t["k"] = batch.tile([P, G * Q_TILES * D], BF16, name="k_sb")
+            nc.sync.dma_start(
+                out=t["k"][:].rearrange("p (t d) -> p t d", d=D),
+                in_=kg[b].rearrange("g (i p) d -> p (g i) d", p=P),
+            )
+            t["q"] = batch.tile([P, H * Q_TILES * D], BF16, name="q_sb")
+            nc.sync.dma_start(
+                out=t["q"][:].rearrange("p (t d) -> p t d", d=D),
+                in_=q[b].rearrange("h (i p) d -> p (h i) d", p=P),
+            )
+            t["kT"] = batch.tile([P, G * S], BF16, name="kT")
+            t["qT"] = batch.tile([P, H * S], BF16, name="qT")
+            t["x_codes"] = batch.tile([P, (S // P) * E_PASSES * P], U32, name="x_codes", align_bytes=64)
+            t["x_scales"] = batch.tile([P, (S // P) * E_PASSES * P], U8, name="x_scales", align_bytes=64)
+            t["v_codes"] = batch.tile([P, G * KEY_PASSES * D], U32, name="v_codes", align_bytes=64)
+            t["v_scales"] = batch.tile([P, G * KEY_PASSES * D], U8, name="v_scales", align_bytes=64)
+            return t
+
+        tiles = {0: load_batch(0)}
+
+        w_raw = consts.tile([P, G * E_PASSES * 2, 2 * D], BF16, name="w_raw")
+        nc.scalar.dma_start(
+            out=w_raw[:], in_=Wv.rearrange("g (a p e) d -> p (g a) (e d)", p=P, e=2)
+        )
+        bv_all = consts.tile([P, G * D], BF16, name="bv_all")
+        nc.scalar.dma_start(out=bv_all[:], in_=bv.rearrange("g d -> (g d)").partition_broadcast(P))
+        warm = consts.tile([P, 1], F32, name="warm")
+        nc.vector.memset(warm[:], 0.0)
+        nc.scalar.activation(out=warm[:], in_=warm[:], func=ACT.Exp)
+        w_grp = consts.tile([P, E_PASSES * G, D, PACK], BF16, name="w_grp", align_bytes=64)
+        for c in range(E_PASSES):
+            for g in range(G):
+                first = (g * E_PASSES + c) * 2
+                nc.vector.tensor_copy(
+                    out=w_grp[:, c * G + g, :, :].rearrange("p d (u e) -> p d u e", u=2),
+                    in_=w_raw[:, first : first + 2, :].rearrange("p u (e d) -> p d u e", e=2),
+                )
+        w_codes = consts.tile([P, E_PASSES * G * D], U32, name="w_codes", align_bytes=64)
+        w_scales = consts.tile([P, E_PASSES * G * D], U8, name="w_scales", align_bytes=64)
+        nc.vector.quantize_mx(
+            out=w_codes[:].bitcast(FP8X4),
+            scales=w_scales[:],
+            in_=w_grp[:].rearrange("p a d t -> p (a d t)"),
+        )
+
+
+        def x_piece(t, j):
+            held = {}
+            x_words = t["x"][:].bitcast(F32)
+            words = E // 2
+
+            def on_tensor():
+                held["ps"] = psum_t.tile([P, E_PASSES * 2, P], F32, name="xt_ps", tag="t")
+                for cu in range(E_PASSES * 2):
+                    nc.tensor.transpose(
+                        held["ps"][:, cu, :],
+                        x_words[:, j * words + cu * P : j * words + (cu + 1) * P],
+                        ident_f[:],
+                    )
+
+            def out_of_psum():
+                held["grp"] = work.tile([P, E_PASSES * K_PASS], BF16, name="x_grp", align_bytes=64)
+                nc.scalar.copy(
+                    out=held["grp"][:].bitcast(F32).rearrange("p (c s u) -> p c s u", c=E_PASSES, u=2),
+                    in_=held["ps"][:].rearrange("p (c u) s -> p c s u", u=2),
+                )
+
+            def quantise():
+                cols = slice(j * E_PASSES * P, (j + 1) * E_PASSES * P)
+                nc.vector.quantize_mx(
+                    out=t["x_codes"][:, cols].bitcast(FP8X4),
+                    scales=t["x_scales"][:, cols],
+                    in_=held["grp"][:],
+                )
+
+            return on_tensor, out_of_psum, quantise
+
+        def v_piece(t, kp, g):
+            held = {}
+
+            def on_tensor():
+                held["ps"] = psum_t.tile([P, TILES_PER_PASS, D], F32, name="v_ps", tag="t")
+                for tt in range(TILES_PER_PASS):
+                    j = kp * TILES_PER_PASS + tt
+                    for c in range(E_PASSES):
+                        x_cols = slice((j * E_PASSES + c) * P, (j * E_PASSES + c + 1) * P)
+                        w_cols = slice((c * G + g) * D, (c * G + g + 1) * D)
+                        nc.tensor.matmul_mx(
+                            out=held["ps"][:, tt, :],
+                            lhsT=t["x_codes"][:, x_cols].bitcast(FP8X4),
+                            lhsT_scale=t["x_scales"][:, x_cols],
+                            rhs=w_codes[:, w_cols].bitcast(FP8X4),
+                            rhs_scale=w_scales[:, w_cols],
+                            start=(c == 0),
+                            stop=(c == E_PASSES - 1),
+                        )
+
+            def out_of_psum():
+                held["grp"] = work.tile([P, D * PACK], BF16, name="v_grp", align_bytes=64)
+                nc.vector.tensor_tensor(
+                    out=held["grp"][:].rearrange("p (d t) -> p d t", t=PACK),
+                    in0=held["ps"][:].rearrange("p t d -> p d t"),
+                    in1=bv_all[:, g * D : (g + 1) * D].unsqueeze(2).to_broadcast([P, D, PACK]),
+                    op=ALU.add,
+                )
+
+            def quantise():
+                cols = slice((g * KEY_PASSES + kp) * D, (g * KEY_PASSES + kp + 1) * D)
+                nc.vector.quantize_mx(
+                    out=t["v_codes"][:, cols].bitcast(FP8X4),
+                    scales=t["v_scales"][:, cols],
+                    in_=held["grp"][:],
+                )
+
+            return on_tensor, out_of_psum, quantise
+
+        def head_piece(rows, transposed, n):
+            held = {}
+
+            def on_tensor():
+                held["ps"] = psum_t.tile([P, S], BF16, name="hT_ps", tag="t")
+                for i in range(Q_TILES):
+                    nc.tensor.transpose(
+                        held["ps"][:, i * P : (i + 1) * P],
+                        rows[:, (n * Q_TILES + i) * D : (n * Q_TILES + i + 1) * D],
+                        ident_bf[:],
+                    )
+
+            def out_of_psum():
+                nc.scalar.copy(out=transposed[:, n * S : (n + 1) * S], in_=held["ps"][:])
+
+            return on_tensor, out_of_psum, None
+
+        def pieces_of(t):
+            pieces = [x_piece(t, j) for j in range(S // P)]
+            pieces += [v_piece(t, kp, g) for kp in range(KEY_PASSES) for g in range(G)]
+            pieces += [head_piece(t["k"], t["kT"], g) for g in range(G)]
+            pieces += [head_piece(t["q"], t["qT"], h) for h in range(H)]
+            return pieces
+
+        def run_piece(pieces, m):
+            if 0 <= m < len(pieces):
+                pieces[m][0]()
+                pieces[m][1]()
+            if 0 <= m - 1 < len(pieces) and pieces[m - 1][2] is not None:
+                pieces[m - 1][2]()
+
+        pieces = pieces_of(tiles[0])
+        for m in range(len(pieces) + 1):
+            run_piece(pieces, m)
+
+        steps = [(b, i, h) for b in range(B) for i in reversed(range(Q_TILES)) for h in range(H)]
+        state = [{} for step in steps]
+        shared = {}
+
+        def shape_of(i):
+            return i // TILES_PER_PASS + 1, i % TILES_PER_PASS
+
+        def width_of(i, c):
+            passes, r = shape_of(i)
+            return K_PASS if c < passes - 1 else (r + 1) * P
+
+        def scores(n):
+            b, i, h = steps[n]
+            passes, r = shape_of(i)
+            g = h // HEADS_PER_GROUP
+            q_cols = tiles[b]["qT"][:, h * S + i * P : h * S + (i + 1) * P]
+            kT = tiles[b]["kT"]
+            state[n]["s"] = []
+            for c in range(passes):
+                s_ps = psum_s.tile([P, K_PASS], F32, name="s_ps", tag="s")
+                state[n]["s"].append(s_ps)
+                key0 = g * S + c * K_PASS
+                below = width_of(i, c) if c < passes - 1 else r * P
+                if below > 0:
+                    nc.tensor.matmul(
+                        s_ps[:, :below], lhsT=q_cols, rhs=kT[:, key0 : key0 + below], start=True, stop=True
+                    )
+                if c == passes - 1:
+                    block = slice(below, below + P)
+                    nc.tensor.matmul(
+                        s_ps[:, block],
+                        lhsT=q_cols,
+                        rhs=kT[:, key0 + below : key0 + below + P],
+                        start=True,
+                        stop=False,
+                    )
+                    nc.tensor.matmul(s_ps[:, block], lhsT=ident_bf[:], rhs=mask_bf[:], start=False, stop=True)
+
+        def rowmax(n):
+            b, i, h = steps[n]
+            passes, r = shape_of(i)
+            top = small.tile([P, passes], F32, name="top")
+            for c in range(passes):
+                nc.vector.tensor_reduce(
+                    out=top[:, c : c + 1], in_=state[n]["s"][c][:, : width_of(i, c)], axis=AX.X, op=ALU.max
+                )
+            shift = small.tile([P, 1], F32, name="shift")
+            if passes == 2:
+                nc.vector.tensor_scalar(
+                    out=shift[:], in0=top[:, 0:1], scalar1=top[:, 1:2], scalar2=-SCALE, op0=ALU.max, op1=ALU.mult
+                )
+            else:
+                nc.vector.tensor_scalar(out=shift[:], in0=top[:, 0:1], scalar1=-SCALE, scalar2=None, op0=ALU.mult)
+            state[n]["shift"] = shift
+
+        def exponential(n):
+            b, i, h = steps[n]
+            passes, r = shape_of(i)
+            if h == 0:
+                shared[(b, i)] = {"sums": small.tile([P, H, passes], F32, name="sums")}
+            sums = shared[(b, i)]["sums"]
+            state[n]["e_words"] = []
+            for c in range(passes):
+                if c < passes - 1:
+                    e_full = ring.tile([P, K_PASS], BF16, name="e_full")
+                    e_sb = e_full[:]
+                    e_words = e_full[:].bitcast(F32)
+                else:
+                    first = (r * H + h) * K_PASS
+                    e_sb = e_diag[:, first : first + K_PASS]
+                    e_words = e_diag[:].bitcast(F32)[:, first // 2 : (first + K_PASS) // 2]
+                state[n]["e_words"].append(e_words)
+                width = width_of(i, c)
+                nc.scalar.activation(
+                    out=e_sb[:, :width],
+                    in_=state[n]["s"][c][:, :width],
+                    func=ACT.Exp,
+                    bias=state[n]["shift"][:],
+                    scale=SCALE,
+                    accum_out=sums[:, h, c : c + 1],
+                )
+
+        def transposes(n):
+            b, i, h = steps[n]
+            passes, r = shape_of(i)
+            et_ps = psum_t.tile([P, passes * 2, P], F32, name="et_ps", tag="t")
+            for c in range(passes):
+                e_words = state[n]["e_words"][c]
+                for u in range(2):
+                    nc.tensor.transpose(et_ps[:, c * 2 + u, :], e_words[:, u * P : (u + 1) * P], ident_f[:])
+            state[n]["et_ps"] = et_ps
+
+        def out_of_psum(n):
+            b, i, h = steps[n]
+            passes, r = shape_of(i)
+            e_grp = work.tile([P, passes * K_PASS], BF16, name="e_grp", align_bytes=64)
+            nc.scalar.copy(
+                out=e_grp[:].bitcast(F32).rearrange("p (c s u) -> p c s u", c=passes, u=2),
+                in_=state[n]["et_ps"][:].rearrange("p (c u) s -> p c s u", u=2),
+            )
+            state[n]["e_grp"] = e_grp
+
+        def quantise(n):
+            b, i, h = steps[n]
+            passes, r = shape_of(i)
+            e_codes = ring.tile([P, passes * P], U32, name="e_codes", align_bytes=64)
+            e_scales = ring.tile([P, passes * P], U8, name="e_scales", align_bytes=64)
+            nc.vector.quantize_mx(out=e_codes[:].bitcast(FP8X4), scales=e_scales[:], in_=state[n]["e_grp"][:])
+            state[n]["e_codes"] = e_codes
+            state[n]["e_scales"] = e_scales
+
+        def weighted_values(n):
+            b, i, h = steps[n]
+            passes, r = shape_of(i)
+            g = h // HEADS_PER_GROUP
+            if h == 0:
+                shared[(b, i)]["o_ps"] = psum_o.tile([P, H * D], F32, name="o_ps", tag="o")
+            o_ps = shared[(b, i)]["o_ps"]
+            for c in range(passes):
+                e_cols = slice(c * P, (c + 1) * P)
+                v_cols = slice((g * KEY_PASSES + c) * D, (g * KEY_PASSES + c + 1) * D)
+                nc.tensor.matmul_mx(
+                    out=o_ps[:, h * D : (h + 1) * D],
+                    lhsT=state[n]["e_codes"][:, e_cols].bitcast(FP8X4),
+                    lhsT_scale=state[n]["e_scales"][:, e_cols],
+                    rhs=tiles[b]["v_codes"][:, v_cols].bitcast(FP8X4),
+                    rhs_scale=tiles[b]["v_scales"][:, v_cols],
+                    start=(c == 0),
+                    stop=(c == passes - 1),
+                )
+
+        def normalise_and_store(n):
+            b, i, h = steps[n]
+            if h < H - 1:
+                return
+            passes, r = shape_of(i)
+            sums = shared[(b, i)]["sums"]
+            total = small.tile([P, H], F32, name="total")
+            nc.vector.tensor_reduce(out=total[:], in_=sums[:], axis=AX.X, op=ALU.add)
+            inverse = small.tile([P, H], F32, name="inverse")
+            nc.vector.reciprocal(out=inverse[:], in_=total[:])
+            o_sb = work.tile([P, H * D], F32, name="o_sb")
+            nc.vector.tensor_tensor(
+                out=o_sb[:].rearrange("p (h d) -> p h d", h=H),
+                in0=shared[(b, i)]["o_ps"][:].rearrange("p (h d) -> p h d", h=H),
+                in1=inverse[:].unsqueeze(2).to_broadcast([P, H, D]),
+                op=ALU.mult,
+            )
+            nc.sync.dma_start(out=out[b, i * P : (i + 1) * P, :], in_=o_sb[:])
+
+        def at(stage, n):
+            if 0 <= n < len(steps):
+                stage(n)
+
+        steps_per_batch = Q_TILES * H
+        LAST_LAG = 5
+        for k in range(len(steps) + LAST_LAG):
+            b_next = k // steps_per_batch + 1
+            if k % steps_per_batch == 0 and b_next < B:
+                tiles[b_next] = load_batch(b_next)
+                pieces = pieces_of(tiles[b_next])
+            at(scores, k)
+            at(rowmax, k)
+            at(exponential, k - 1)
+            at(transposes, k - 2)
+            at(out_of_psum, k - 2)
+            at(quantise, k - 3)
+            if b_next < B:
+                run_piece(pieces, k % steps_per_batch)
+            at(weighted_values, k - 4)
+            at(normalise_and_store, k - LAST_LAG)

@@ -11,7 +11,6 @@ U8 = mybir.dt.uint8
 FP8X4 = mybir.dt.float8_e4m3fn_x4
 ALU = mybir.AluOpType
 ACT = mybir.ActivationFunctionType
-AX = mybir.AxisListType
 
 B, S, E, H, G, D = 4, 1024, 1024, 4, 2, 128
 P = 128
@@ -24,6 +23,7 @@ KEY_PASSES = S // K_PASS
 HEADS_PER_GROUP = H // G
 SCALE = 1.0 / math.sqrt(D)
 MASKED = -(2.0**100)
+PV_LAG = 14
 
 FLOPS = 2 * B * G * S * E * D + 2 * 2 * B * H * D * (K_PASS * K_PASS + K_PASS * S)
 
@@ -35,11 +35,11 @@ def tile_multiheadattention_pa_t_kernel(tc, q, kg, x, Wv, bv, out):
         batch = ctx.enter_context(tc.tile_pool(name="batch", bufs=2))
         work = ctx.enter_context(tc.tile_pool(name="work", bufs=3))
         ring = ctx.enter_context(tc.tile_pool(name="ring", bufs=4))
+        waiting = ctx.enter_context(tc.tile_pool(name="waiting", bufs=PV_LAG))
         small = ctx.enter_context(tc.tile_pool(name="small", bufs=6))
         psum_s = ctx.enter_context(tc.psum_pool(name="psum_s", bufs=4))
         psum_t = ctx.enter_context(tc.psum_pool(name="psum_t", bufs=2))
         psum_o = ctx.enter_context(tc.psum_pool(name="psum_o", bufs=2))
-        ctx.enter_context(tc.manual_schedule())
 
         ident_f = consts.tile([P, P], F32, name="ident_f")
         make_identity(nc, ident_f[:])
@@ -59,13 +59,33 @@ def tile_multiheadattention_pa_t_kernel(tc, q, kg, x, Wv, bv, out):
         mask_bf = consts.tile([P, P], BF16, name="mask_bf")
         nc.vector.tensor_copy(out=mask_bf[:], in_=mask_f[:])
 
-        e_diag = consts.tile([P, TILES_PER_PASS * H * K_PASS], BF16, name="e_diag")
-        e_diag_view = e_diag[:].rearrange("p (r h k) -> p r h k", r=TILES_PER_PASS, h=H)
+        e_rows = consts.tile([P, TILES_PER_PASS * H * S], BF16, name="e_rows")
+        e_rows_view = e_rows[:].rearrange("p (r h k) -> p r h k", r=TILES_PER_PASS, h=H)
         for r in range(TILES_PER_PASS - 1):
-            nc.vector.memset(e_diag_view[:, r, :, (r + 1) * P :], 0.0)
+            nc.vector.memset(e_rows_view[:, r, :, S - K_PASS + (r + 1) * P :], 0.0)
 
-        def load_batch(b):
-            t = {}
+        tiles = [{} for b in range(B)]
+
+        def load_heads(b):
+            t = tiles[b]
+            t["k"] = batch.tile([P, G * Q_TILES * D], BF16, name="k_sb")
+            t["q"] = batch.tile([P, H * Q_TILES * D], BF16, name="q_sb")
+            width = Q_TILES * D
+            for g in range(G):
+                nc.sync.dma_start(
+                    out=t["k"][:, g * width : (g + 1) * width].rearrange("p (i d) -> p i d", d=D),
+                    in_=kg[b, g].rearrange("(i p) d -> p i d", p=P),
+                )
+                for h in range(g * HEADS_PER_GROUP, (g + 1) * HEADS_PER_GROUP):
+                    nc.sync.dma_start(
+                        out=t["q"][:, h * width : (h + 1) * width].rearrange("p (i d) -> p i d", d=D),
+                        in_=q[b, h].rearrange("(i p) d -> p i d", p=P),
+                    )
+            t["kT"] = batch.tile([P, G * S], BF16, name="kT")
+            t["qT"] = batch.tile([P, H * S], BF16, name="qT")
+
+        def load_x(b):
+            t = tiles[b]
             t["x"] = batch.tile([P, (S // P) * E], BF16, name="x_sb")
             rows = 2 * P
             for a in range(S // rows):
@@ -73,25 +93,13 @@ def tile_multiheadattention_pa_t_kernel(tc, q, kg, x, Wv, bv, out):
                     out=t["x"][:, a * 2 * E : (a + 1) * 2 * E],
                     in_=x[b, a * rows : (a + 1) * rows, :].rearrange("(p e) k -> p (e k)", e=2),
                 )
-            t["k"] = batch.tile([P, G * Q_TILES * D], BF16, name="k_sb")
-            nc.sync.dma_start(
-                out=t["k"][:].rearrange("p (t d) -> p t d", d=D),
-                in_=kg[b].rearrange("g (i p) d -> p (g i) d", p=P),
-            )
-            t["q"] = batch.tile([P, H * Q_TILES * D], BF16, name="q_sb")
-            nc.sync.dma_start(
-                out=t["q"][:].rearrange("p (t d) -> p t d", d=D),
-                in_=q[b].rearrange("h (i p) d -> p (h i) d", p=P),
-            )
-            t["kT"] = batch.tile([P, G * S], BF16, name="kT")
-            t["qT"] = batch.tile([P, H * S], BF16, name="qT")
             t["x_codes"] = batch.tile([P, (S // P) * E_PASSES * P], U32, name="x_codes", align_bytes=64)
             t["x_scales"] = batch.tile([P, (S // P) * E_PASSES * P], U8, name="x_scales", align_bytes=64)
             t["v_codes"] = batch.tile([P, G * KEY_PASSES * D], U32, name="v_codes", align_bytes=64)
             t["v_scales"] = batch.tile([P, G * KEY_PASSES * D], U8, name="v_scales", align_bytes=64)
-            return t
 
-        tiles = {0: load_batch(0)}
+        load_heads(0)
+        load_x(0)
 
         w_raw = consts.tile([P, G * E_PASSES * 2, 2 * D], BF16, name="w_raw")
         nc.scalar.dma_start(
@@ -135,7 +143,8 @@ def tile_multiheadattention_pa_t_kernel(tc, q, kg, x, Wv, bv, out):
 
             def out_of_psum():
                 held["grp"] = work.tile([P, E_PASSES * K_PASS], BF16, name="x_grp", align_bytes=64)
-                nc.scalar.copy(
+                copy = nc.scalar.copy if j % 2 == 0 else nc.vector.tensor_copy
+                copy(
                     out=held["grp"][:].bitcast(F32).rearrange("p (c s u) -> p c s u", c=E_PASSES, u=2),
                     in_=held["ps"][:].rearrange("p (c u) s -> p c s u", u=2),
                 )
@@ -206,11 +215,17 @@ def tile_multiheadattention_pa_t_kernel(tc, q, kg, x, Wv, bv, out):
 
             return on_tensor, out_of_psum, None
 
-        def pieces_of(t):
+        def value_pieces(t):
             pieces = [x_piece(t, j) for j in range(S // P)]
             pieces += [v_piece(t, kp, g) for kp in range(KEY_PASSES) for g in range(G)]
-            pieces += [head_piece(t["k"], t["kT"], g) for g in range(G)]
-            pieces += [head_piece(t["q"], t["qT"], h) for h in range(H)]
+            return pieces
+
+        def head_pieces(t):
+            pieces = []
+            for g in range(G):
+                pieces.append(head_piece(t["k"], t["kT"], g))
+                for h in range(g * HEADS_PER_GROUP, (g + 1) * HEADS_PER_GROUP):
+                    pieces.append(head_piece(t["q"], t["qT"], h))
             return pieces
 
         def run_piece(pieces, m):
@@ -220,8 +235,8 @@ def tile_multiheadattention_pa_t_kernel(tc, q, kg, x, Wv, bv, out):
             if 0 <= m - 1 < len(pieces) and pieces[m - 1][2] is not None:
                 pieces[m - 1][2]()
 
-        pieces = pieces_of(tiles[0])
-        for m in range(len(pieces) + 1):
+        pieces = head_pieces(tiles[0])
+        for m in range(len(pieces)):
             run_piece(pieces, m)
 
         steps = [(b, i, h) for b in range(B) for i in reversed(range(Q_TILES)) for h in range(H)]
@@ -265,55 +280,45 @@ def tile_multiheadattention_pa_t_kernel(tc, q, kg, x, Wv, bv, out):
         def rowmax(n):
             b, i, h = steps[n]
             passes, r = shape_of(i)
-            top = small.tile([P, passes], F32, name="top")
+            lowest = small.tile([P, passes], F32, name="lowest")
+            minus_s = ring.tile([P, passes * K_PASS], F32, name="minus_s")
             for c in range(passes):
-                nc.vector.tensor_reduce(
-                    out=top[:, c : c + 1], in_=state[n]["s"][c][:, : width_of(i, c)], axis=AX.X, op=ALU.max
-                )
-            shift = small.tile([P, 1], F32, name="shift")
-            if passes == 2:
+                width = width_of(i, c)
                 nc.vector.tensor_scalar(
-                    out=shift[:], in0=top[:, 0:1], scalar1=top[:, 1:2], scalar2=-SCALE, op0=ALU.max, op1=ALU.mult
+                    out=minus_s[:, c * K_PASS : c * K_PASS + width],
+                    in0=state[n]["s"][c][:, :width],
+                    scalar1=-SCALE,
+                    scalar2=(lowest[:, c - 1 : c] if c > 0 else None),
+                    op0=ALU.mult,
+                    op1=ALU.min,
+                    accum_out=lowest[:, c : c + 1],
                 )
-            else:
-                nc.vector.tensor_scalar(out=shift[:], in0=top[:, 0:1], scalar1=-SCALE, scalar2=None, op0=ALU.mult)
-            state[n]["shift"] = shift
+            state[n]["minus_s"] = minus_s
+            state[n]["shift"] = lowest[:, passes - 1 : passes]
 
         def exponential(n):
             b, i, h = steps[n]
             passes, r = shape_of(i)
             if h == 0:
-                shared[(b, i)] = {"sums": small.tile([P, H, passes], F32, name="sums")}
-            sums = shared[(b, i)]["sums"]
-            state[n]["e_words"] = []
-            for c in range(passes):
-                if c < passes - 1:
-                    e_full = ring.tile([P, K_PASS], BF16, name="e_full")
-                    e_sb = e_full[:]
-                    e_words = e_full[:].bitcast(F32)
-                else:
-                    first = (r * H + h) * K_PASS
-                    e_sb = e_diag[:, first : first + K_PASS]
-                    e_words = e_diag[:].bitcast(F32)[:, first // 2 : (first + K_PASS) // 2]
-                state[n]["e_words"].append(e_words)
-                width = width_of(i, c)
-                nc.scalar.activation(
-                    out=e_sb[:, :width],
-                    in_=state[n]["s"][c][:, :width],
-                    func=ACT.Exp,
-                    bias=state[n]["shift"][:],
-                    scale=SCALE,
-                    accum_out=sums[:, h, c : c + 1],
-                )
+                shared[(b, i)] = {"sums": waiting.tile([P, H], F32, name="sums")}
+            first = (r * H + h + 1) * S - passes * K_PASS
+            width = (i + 1) * P
+            nc.scalar.activation(
+                out=e_rows[:, first : first + width],
+                in_=state[n]["minus_s"][:, :width],
+                func=ACT.Exp,
+                bias=state[n]["shift"],
+                scale=-1.0,
+                accum_out=shared[(b, i)]["sums"][:, h : h + 1],
+            )
+            state[n]["e_words"] = e_rows[:].bitcast(F32)[:, first // 2 : first // 2 + passes * K_PASS // 2]
 
         def transposes(n):
             b, i, h = steps[n]
             passes, r = shape_of(i)
             et_ps = psum_t.tile([P, passes * 2, P], F32, name="et_ps", tag="t")
-            for c in range(passes):
-                e_words = state[n]["e_words"][c]
-                for u in range(2):
-                    nc.tensor.transpose(et_ps[:, c * 2 + u, :], e_words[:, u * P : (u + 1) * P], ident_f[:])
+            for cu in range(passes * 2):
+                nc.tensor.transpose(et_ps[:, cu, :], state[n]["e_words"][:, cu * P : (cu + 1) * P], ident_f[:])
             state[n]["et_ps"] = et_ps
 
         def out_of_psum(n):
@@ -329,8 +334,8 @@ def tile_multiheadattention_pa_t_kernel(tc, q, kg, x, Wv, bv, out):
         def quantise(n):
             b, i, h = steps[n]
             passes, r = shape_of(i)
-            e_codes = ring.tile([P, passes * P], U32, name="e_codes", align_bytes=64)
-            e_scales = ring.tile([P, passes * P], U8, name="e_scales", align_bytes=64)
+            e_codes = waiting.tile([P, passes * P], U32, name="e_codes", align_bytes=64)
+            e_scales = waiting.tile([P, passes * P], U8, name="e_scales", align_bytes=64)
             nc.vector.quantize_mx(out=e_codes[:].bitcast(FP8X4), scales=e_scales[:], in_=state[n]["e_grp"][:])
             state[n]["e_codes"] = e_codes
             state[n]["e_scales"] = e_scales
@@ -359,12 +364,8 @@ def tile_multiheadattention_pa_t_kernel(tc, q, kg, x, Wv, bv, out):
             b, i, h = steps[n]
             if h < H - 1:
                 return
-            passes, r = shape_of(i)
-            sums = shared[(b, i)]["sums"]
-            total = small.tile([P, H], F32, name="total")
-            nc.vector.tensor_reduce(out=total[:], in_=sums[:], axis=AX.X, op=ALU.add)
             inverse = small.tile([P, H], F32, name="inverse")
-            nc.vector.reciprocal(out=inverse[:], in_=total[:])
+            nc.vector.reciprocal(out=inverse[:], in_=shared[(b, i)]["sums"][:])
             o_sb = work.tile([P, H * D], F32, name="o_sb")
             nc.vector.tensor_tensor(
                 out=o_sb[:].rearrange("p (h d) -> p h d", h=H),
@@ -379,19 +380,21 @@ def tile_multiheadattention_pa_t_kernel(tc, q, kg, x, Wv, bv, out):
                 stage(n)
 
         steps_per_batch = Q_TILES * H
-        LAST_LAG = 5
-        for k in range(len(steps) + LAST_LAG):
-            b_next = k // steps_per_batch + 1
-            if k % steps_per_batch == 0 and b_next < B:
-                tiles[b_next] = load_batch(b_next)
-                pieces = pieces_of(tiles[b_next])
+        for k in range(len(steps) + PV_LAG + 1):
+            b_now = k // steps_per_batch
+            if k % steps_per_batch == 0 and b_now < B:
+                pieces = value_pieces(tiles[b_now])
+                if b_now + 1 < B:
+                    load_heads(b_now + 1)
+                    load_x(b_now + 1)
+                    pieces += head_pieces(tiles[b_now + 1])
             at(scores, k)
-            at(rowmax, k)
-            at(exponential, k - 1)
-            at(transposes, k - 2)
-            at(out_of_psum, k - 2)
-            at(quantise, k - 3)
-            if b_next < B:
+            at(rowmax, k - 1)
+            at(exponential, k - 2)
+            at(transposes, k - 3)
+            at(out_of_psum, k - 3)
+            at(quantise, k - 4)
+            if b_now < B:
                 run_piece(pieces, k % steps_per_batch)
-            at(weighted_values, k - 4)
-            at(normalise_and_store, k - LAST_LAG)
+            at(weighted_values, k - PV_LAG)
+            at(normalise_and_store, k - PV_LAG - 1)

@@ -23,7 +23,7 @@ KEY_PASSES = S // K_PASS
 HEADS_PER_GROUP = H // G
 SCALE = 1.0 / math.sqrt(D)
 MASKED = -(2.0**100)
-PV_LAG = 14
+PV_LAG = 10
 
 FLOPS = 2 * B * G * S * E * D + 2 * 2 * B * H * D * (K_PASS * K_PASS + K_PASS * S)
 
@@ -35,7 +35,7 @@ def tile_multiheadattention_pa_t_kernel(tc, q, kg, x, Wv, bv, out):
         batch = ctx.enter_context(tc.tile_pool(name="batch", bufs=2))
         work = ctx.enter_context(tc.tile_pool(name="work", bufs=3))
         ring = ctx.enter_context(tc.tile_pool(name="ring", bufs=4))
-        waiting = ctx.enter_context(tc.tile_pool(name="waiting", bufs=PV_LAG))
+        wide = ctx.enter_context(tc.tile_pool(name="wide", bufs=3))
         small = ctx.enter_context(tc.tile_pool(name="small", bufs=6))
         psum_s = ctx.enter_context(tc.psum_pool(name="psum_s", bufs=4))
         psum_t = ctx.enter_context(tc.psum_pool(name="psum_t", bufs=2))
@@ -300,7 +300,7 @@ def tile_multiheadattention_pa_t_kernel(tc, q, kg, x, Wv, bv, out):
             b, i, h = steps[n]
             passes, r = shape_of(i)
             if h == 0:
-                shared[(b, i)] = {"sums": waiting.tile([P, H], F32, name="sums")}
+                shared[(b, i)] = {"sums": small.tile([P, H], F32, name="sums")}
             first = (r * H + h + 1) * S - passes * K_PASS
             width = (i + 1) * P
             nc.scalar.activation(
@@ -324,46 +324,47 @@ def tile_multiheadattention_pa_t_kernel(tc, q, kg, x, Wv, bv, out):
         def out_of_psum(n):
             b, i, h = steps[n]
             passes, r = shape_of(i)
-            e_grp = work.tile([P, passes * K_PASS], BF16, name="e_grp", align_bytes=64)
+            width = passes * K_PASS
+            if h == 0:
+                shared[(b, i)]["e_grp"] = wide.tile([P, H * width], BF16, name="e_grp", align_bytes=64)
+            e_grp = shared[(b, i)]["e_grp"]
             nc.scalar.copy(
-                out=e_grp[:].bitcast(F32).rearrange("p (c s u) -> p c s u", c=passes, u=2),
+                out=e_grp[:].bitcast(F32)[:, h * width // 2 : (h + 1) * width // 2].rearrange(
+                    "p (c s u) -> p c s u", c=passes, u=2
+                ),
                 in_=state[n]["et_ps"][:].rearrange("p (c u) s -> p c s u", u=2),
             )
-            state[n]["e_grp"] = e_grp
 
-        def quantise(n):
-            b, i, h = steps[n]
+        def quantise(b, i):
             passes, r = shape_of(i)
-            e_codes = waiting.tile([P, passes * P], U32, name="e_codes", align_bytes=64)
-            e_scales = waiting.tile([P, passes * P], U8, name="e_scales", align_bytes=64)
-            nc.vector.quantize_mx(out=e_codes[:].bitcast(FP8X4), scales=e_scales[:], in_=state[n]["e_grp"][:])
-            state[n]["e_codes"] = e_codes
-            state[n]["e_scales"] = e_scales
+            e_codes = wide.tile([P, H * passes * P], U32, name="e_codes", align_bytes=64)
+            e_scales = wide.tile([P, H * passes * P], U8, name="e_scales", align_bytes=64)
+            nc.vector.quantize_mx(
+                out=e_codes[:].bitcast(FP8X4), scales=e_scales[:], in_=shared[(b, i)]["e_grp"][:]
+            )
+            shared[(b, i)]["e_codes"] = e_codes
+            shared[(b, i)]["e_scales"] = e_scales
 
-        def weighted_values(n):
-            b, i, h = steps[n]
+        def weighted_values(b, i):
             passes, r = shape_of(i)
-            g = h // HEADS_PER_GROUP
-            if h == 0:
-                shared[(b, i)]["o_ps"] = psum_o.tile([P, H * D], F32, name="o_ps", tag="o")
-            o_ps = shared[(b, i)]["o_ps"]
-            for c in range(passes):
-                e_cols = slice(c * P, (c + 1) * P)
-                v_cols = slice((g * KEY_PASSES + c) * D, (g * KEY_PASSES + c + 1) * D)
-                nc.tensor.matmul_mx(
-                    out=o_ps[:, h * D : (h + 1) * D],
-                    lhsT=state[n]["e_codes"][:, e_cols].bitcast(FP8X4),
-                    lhsT_scale=state[n]["e_scales"][:, e_cols],
-                    rhs=tiles[b]["v_codes"][:, v_cols].bitcast(FP8X4),
-                    rhs_scale=tiles[b]["v_scales"][:, v_cols],
-                    start=(c == 0),
-                    stop=(c == passes - 1),
-                )
+            o_ps = psum_o.tile([P, H * D], F32, name="o_ps", tag="o")
+            for h in range(H):
+                g = h // HEADS_PER_GROUP
+                for c in range(passes):
+                    e_cols = slice((h * passes + c) * P, (h * passes + c + 1) * P)
+                    v_cols = slice((g * KEY_PASSES + c) * D, (g * KEY_PASSES + c + 1) * D)
+                    nc.tensor.matmul_mx(
+                        out=o_ps[:, h * D : (h + 1) * D],
+                        lhsT=shared[(b, i)]["e_codes"][:, e_cols].bitcast(FP8X4),
+                        lhsT_scale=shared[(b, i)]["e_scales"][:, e_cols],
+                        rhs=tiles[b]["v_codes"][:, v_cols].bitcast(FP8X4),
+                        rhs_scale=tiles[b]["v_scales"][:, v_cols],
+                        start=(c == 0),
+                        stop=(c == passes - 1),
+                    )
+            shared[(b, i)]["o_ps"] = o_ps
 
-        def normalise_and_store(n):
-            b, i, h = steps[n]
-            if h < H - 1:
-                return
+        def normalise_and_store(b, i):
             inverse = small.tile([P, H], F32, name="inverse")
             nc.vector.reciprocal(out=inverse[:], in_=shared[(b, i)]["sums"][:])
             o_sb = work.tile([P, H * D], F32, name="o_sb")
@@ -379,6 +380,10 @@ def tile_multiheadattention_pa_t_kernel(tc, q, kg, x, Wv, bv, out):
             if 0 <= n < len(steps):
                 stage(n)
 
+        def after_last_head(stage, n):
+            if 0 <= n < len(steps) and steps[n][2] == H - 1:
+                stage(steps[n][0], steps[n][1])
+
         steps_per_batch = Q_TILES * H
         for k in range(len(steps) + PV_LAG + 1):
             b_now = k // steps_per_batch
@@ -393,8 +398,8 @@ def tile_multiheadattention_pa_t_kernel(tc, q, kg, x, Wv, bv, out):
             at(exponential, k - 2)
             at(transposes, k - 3)
             at(out_of_psum, k - 3)
-            at(quantise, k - 4)
+            after_last_head(quantise, k - 4)
             if b_now < B:
                 run_piece(pieces, k % steps_per_batch)
-            at(weighted_values, k - PV_LAG)
-            at(normalise_and_store, k - PV_LAG - 1)
+            after_last_head(weighted_values, k - PV_LAG)
+            after_last_head(normalise_and_store, k - PV_LAG - 1)

@@ -34,12 +34,12 @@ def tile_multiheadattention_pa_t_kernel(tc, q, kg, x, Wv, bv, out):
         consts = ctx.enter_context(tc.tile_pool(name="consts", bufs=1))
         batch = ctx.enter_context(tc.tile_pool(name="batch", bufs=2))
         work = ctx.enter_context(tc.tile_pool(name="work", bufs=3))
-        ring = ctx.enter_context(tc.tile_pool(name="ring", bufs=4))
+        ring = ctx.enter_context(tc.tile_pool(name="ring", bufs=6))
         wide = ctx.enter_context(tc.tile_pool(name="wide", bufs=3))
         small = ctx.enter_context(tc.tile_pool(name="small", bufs=6))
         psum_s = ctx.enter_context(tc.psum_pool(name="psum_s", bufs=4))
-        psum_t = ctx.enter_context(tc.psum_pool(name="psum_t", bufs=2))
-        psum_o = ctx.enter_context(tc.psum_pool(name="psum_o", bufs=2))
+        psum_t = ctx.enter_context(tc.psum_pool(name="psum_t", bufs=3))
+        psum_o = ctx.enter_context(tc.psum_pool(name="psum_o", bufs=1))
 
         ident_f = consts.tile([P, P], F32, name="ident_f")
         make_identity(nc, ident_f[:])
@@ -143,8 +143,7 @@ def tile_multiheadattention_pa_t_kernel(tc, q, kg, x, Wv, bv, out):
 
             def out_of_psum():
                 held["grp"] = work.tile([P, E_PASSES * K_PASS], BF16, name="x_grp", align_bytes=64)
-                copy = nc.scalar.copy if j % 2 == 0 else nc.vector.tensor_copy
-                copy(
+                nc.scalar.copy(
                     out=held["grp"][:].bitcast(F32).rearrange("p (c s u) -> p c s u", c=E_PASSES, u=2),
                     in_=held["ps"][:].rearrange("p (c u) s -> p c s u", u=2),
                 )
@@ -288,13 +287,20 @@ def tile_multiheadattention_pa_t_kernel(tc, q, kg, x, Wv, bv, out):
                     out=minus_s[:, c * K_PASS : c * K_PASS + width],
                     in0=state[n]["s"][c][:, :width],
                     scalar1=-SCALE,
-                    scalar2=(lowest[:, c - 1 : c] if c > 0 else None),
+                    scalar2=None,
                     op0=ALU.mult,
                     op1=ALU.min,
                     accum_out=lowest[:, c : c + 1],
                 )
             state[n]["minus_s"] = minus_s
-            state[n]["shift"] = lowest[:, passes - 1 : passes]
+            if passes == 1:
+                state[n]["shift"] = lowest[:, 0:1]
+            else:
+                shift = small.tile([P, 1], F32, name="shift")
+                nc.gpsimd.tensor_scalar(
+                    out=shift[:], in0=lowest[:, 0:1], scalar1=lowest[:, 1:2], scalar2=None, op0=ALU.min
+                )
+                state[n]["shift"] = shift[:]
 
         def exponential(n):
             b, i, h = steps[n]
@@ -344,6 +350,9 @@ def tile_multiheadattention_pa_t_kernel(tc, q, kg, x, Wv, bv, out):
             )
             shared[(b, i)]["e_codes"] = e_codes
             shared[(b, i)]["e_scales"] = e_scales
+            inverse = small.tile([P, H], F32, name="inverse")
+            nc.vector.reciprocal(out=inverse[:], in_=shared[(b, i)]["sums"][:])
+            shared[(b, i)]["inverse"] = inverse
 
         def weighted_values(b, i):
             passes, r = shape_of(i)
@@ -365,13 +374,11 @@ def tile_multiheadattention_pa_t_kernel(tc, q, kg, x, Wv, bv, out):
             shared[(b, i)]["o_ps"] = o_ps
 
         def normalise_and_store(b, i):
-            inverse = small.tile([P, H], F32, name="inverse")
-            nc.vector.reciprocal(out=inverse[:], in_=shared[(b, i)]["sums"][:])
             o_sb = work.tile([P, H * D], F32, name="o_sb")
             nc.vector.tensor_tensor(
                 out=o_sb[:].rearrange("p (h d) -> p h d", h=H),
                 in0=shared[(b, i)]["o_ps"][:].rearrange("p (h d) -> p h d", h=H),
-                in1=inverse[:].unsqueeze(2).to_broadcast([P, H, D]),
+                in1=shared[(b, i)]["inverse"][:].unsqueeze(2).to_broadcast([P, H, D]),
                 op=ALU.mult,
             )
             nc.sync.dma_start(out=out[b, i * P : (i + 1) * P, :], in_=o_sb[:])

@@ -210,7 +210,9 @@ def tile_multiheadattention_pa_t_kernel(tc, q, kg, x, Wv, bv, out):
                     )
 
             def out_of_psum():
-                nc.scalar.copy(out=transposed[:, n * S : (n + 1) * S], in_=held["ps"][:])
+                nc.scalar.copy(
+                    out=transposed[:, n * S : (n + 1) * S].bitcast(F32), in_=held["ps"][:].bitcast(F32)
+                )
 
             return on_tensor, out_of_psum, None
 

@@ -23,8 +23,10 @@ KEY_PASSES = S // K_PASS
 HEADS_PER_GROUP = H // G
 SCALE = 1.0 / math.sqrt(D)
 MASKED = -(2.0**100)
-PV_LAG = 10
+PV_LAG = 16
 
+ORDER = [('s', 0), ('v', 15), ('t', 3), ('n', 17), ('r', 0), ('c', 3), ('e', 1), ('q', 7), ('p', 0)]
+PLAN = [('x0', 0), ('x1', 1), ('x2', 2), ('x3', 3), ('q2', 4), ('v0', 5), ('v1', 6), ('x4', 7), ('x5', 8), ('x6', 9), ('x7', 10), ('v2', 12), ('v3', 13), ('q1', 14), ('q0', 19), ('K0', 24), ('Q3', 26), ('K1', 28)]
 FLOPS = 2 * B * G * S * E * D + 2 * 2 * B * H * D * (K_PASS * K_PASS + K_PASS * S)
 
 
@@ -34,7 +36,7 @@ def tile_multiheadattention_pa_t_kernel(tc, q, kg, x, Wv, bv, out):
         consts = ctx.enter_context(tc.tile_pool(name="consts", bufs=1))
         batch = ctx.enter_context(tc.tile_pool(name="batch", bufs=2))
         work = ctx.enter_context(tc.tile_pool(name="work", bufs=3))
-        ring = ctx.enter_context(tc.tile_pool(name="ring", bufs=6))
+        ring = ctx.enter_context(tc.tile_pool(name="ring", bufs=4))
         wide = ctx.enter_context(tc.tile_pool(name="wide", bufs=3))
         small = ctx.enter_context(tc.tile_pool(name="small", bufs=6))
         psum_s = ctx.enter_context(tc.psum_pool(name="psum_s", bufs=4))
@@ -70,19 +72,22 @@ def tile_multiheadattention_pa_t_kernel(tc, q, kg, x, Wv, bv, out):
             t = tiles[b]
             t["k"] = batch.tile([P, G * Q_TILES * D], BF16, name="k_sb")
             t["q"] = batch.tile([P, H * Q_TILES * D], BF16, name="q_sb")
-            width = Q_TILES * D
-            for g in range(G):
-                nc.sync.dma_start(
-                    out=t["k"][:, g * width : (g + 1) * width].rearrange("p (i d) -> p i d", d=D),
-                    in_=kg[b, g].rearrange("(i p) d -> p i d", p=P),
-                )
-                for h in range(g * HEADS_PER_GROUP, (g + 1) * HEADS_PER_GROUP):
-                    nc.sync.dma_start(
-                        out=t["q"][:, h * width : (h + 1) * width].rearrange("p (i d) -> p i d", d=D),
-                        in_=q[b, h].rearrange("(i p) d -> p i d", p=P),
-                    )
             t["kT"] = batch.tile([P, G * S], BF16, name="kT")
             t["qT"] = batch.tile([P, H * S], BF16, name="qT")
+
+        def load_k(b, g):
+            width = Q_TILES * D
+            nc.sync.dma_start(
+                out=tiles[b]["k"][:, g * width : (g + 1) * width].rearrange("p (i d) -> p i d", d=D),
+                in_=kg[b, g].rearrange("(i p) d -> p i d", p=P),
+            )
+
+        def load_q(b, i):
+            width = H * D
+            nc.sync.dma_start(
+                out=tiles[b]["q"][:, i * width : (i + 1) * width].rearrange("p (h d) -> p h d", d=D),
+                in_=q[b, :, i * P : (i + 1) * P, :].rearrange("h p d -> p h d"),
+            )
 
         def load_x(b):
             t = tiles[b]
@@ -98,8 +103,17 @@ def tile_multiheadattention_pa_t_kernel(tc, q, kg, x, Wv, bv, out):
             t["v_codes"] = batch.tile([P, G * KEY_PASSES * D], U32, name="v_codes", align_bytes=64)
             t["v_scales"] = batch.tile([P, G * KEY_PASSES * D], U8, name="v_scales", align_bytes=64)
 
-        load_heads(0)
-        load_x(0)
+        def load_batch(b):
+            load_heads(b)
+            load_k(b, 0)
+            load_q(b, Q_TILES - 1)
+            load_q(b, Q_TILES - 2)
+            load_k(b, 1)
+            load_x(b)
+            for i in reversed(range(Q_TILES - 2)):
+                load_q(b, i)
+
+        load_batch(0)
 
         w_raw = consts.tile([P, G * E_PASSES * 2, 2 * D], BF16, name="w_raw")
         nc.scalar.dma_start(
@@ -221,24 +235,28 @@ def tile_multiheadattention_pa_t_kernel(tc, q, kg, x, Wv, bv, out):
             pieces += [v_piece(t, kp, g) for kp in range(KEY_PASSES) for g in range(G)]
             return pieces
 
-        def head_pieces(t):
-            pieces = []
-            for g in range(G):
-                pieces.append(head_piece(t["k"], t["kT"], g))
-                for h in range(g * HEADS_PER_GROUP, (g + 1) * HEADS_PER_GROUP):
-                    pieces.append(head_piece(t["q"], t["qT"], h))
-            return pieces
+        def k_piece(t, g):
+            return head_piece(t["k"], t["kT"], g)
 
-        def run_piece(pieces, m):
-            if 0 <= m < len(pieces):
-                pieces[m][0]()
-                pieces[m][1]()
-            if 0 <= m - 1 < len(pieces) and pieces[m - 1][2] is not None:
-                pieces[m - 1][2]()
+        def q_piece(t, n):
+            return head_piece(t["q"], t["qT"], n)
 
-        pieces = head_pieces(tiles[0])
-        for m in range(len(pieces)):
-            run_piece(pieces, m)
+        steps_per_batch = Q_TILES * H
+        pieces_of_round = {}
+
+        def run_pieces(k):
+            for on_tensor, out_of_psum, quantise in pieces_of_round.get(k, []):
+                on_tensor()
+                out_of_psum()
+            for on_tensor, out_of_psum, quantise in pieces_of_round.get(k - 1, []):
+                if quantise is not None:
+                    quantise()
+
+        ctx.enter_context(tc.manual_schedule())
+        for on_tensor, out_of_psum, quantise in (k_piece(tiles[0], 0), q_piece(tiles[0], 3)):
+            on_tensor()
+            out_of_psum()
+        pieces_of_round[0] = [k_piece(tiles[0], 1)]
 
         steps = [(b, i, h) for b in range(B) for i in reversed(range(Q_TILES)) for h in range(H)]
         state = [{} for step in steps]
@@ -255,7 +273,7 @@ def tile_multiheadattention_pa_t_kernel(tc, q, kg, x, Wv, bv, out):
             b, i, h = steps[n]
             passes, r = shape_of(i)
             g = h // HEADS_PER_GROUP
-            q_cols = tiles[b]["qT"][:, h * S + i * P : h * S + (i + 1) * P]
+            q_cols = tiles[b]["qT"][:, (i * H + h) * P : (i * H + h + 1) * P]
             kT = tiles[b]["kT"]
             state[n]["s"] = []
             for c in range(passes):
@@ -393,22 +411,27 @@ def tile_multiheadattention_pa_t_kernel(tc, q, kg, x, Wv, bv, out):
             if 0 <= n < len(steps) and steps[n][2] == H - 1:
                 stage(steps[n][0], steps[n][1])
 
-        steps_per_batch = Q_TILES * H
         for k in range(len(steps) + PV_LAG + 1):
             b_now = k // steps_per_batch
             if k % steps_per_batch == 0 and b_now < B:
-                pieces = value_pieces(tiles[b_now])
+                x0, x1, x2, x3, x4, x5, x6, x7, v00, v01, v10, v11 = value_pieces(tiles[b_now])
+                own = {"x0": x0, "x1": x1, "x2": x2, "x3": x3, "x4": x4, "x5": x5, "x6": x6, "x7": x7}
+                own.update({"v0": v00, "v1": v01, "v2": v10, "v3": v11})
+                own.update({"q2": q_piece(tiles[b_now], 2), "q1": q_piece(tiles[b_now], 1), "q0": q_piece(tiles[b_now], 0)})
                 if b_now + 1 < B:
-                    load_heads(b_now + 1)
-                    load_x(b_now + 1)
-                    pieces += head_pieces(tiles[b_now + 1])
-            at(scores, k)
-            at(rowmax, k - 1)
-            at(exponential, k - 2)
-            at(transposes, k - 3)
-            at(out_of_psum, k - 3)
-            after_last_head(quantise, k - 4)
-            if b_now < B:
-                run_piece(pieces, k % steps_per_batch)
-            after_last_head(weighted_values, k - PV_LAG)
-            after_last_head(normalise_and_store, k - PV_LAG - 1)
+                    load_batch(b_now + 1)
+                    nt = tiles[b_now + 1]
+                    own.update({"K0": k_piece(nt, 0), "Q3": q_piece(nt, 3), "K1": k_piece(nt, 1)})
+                for name, rnd in PLAN:
+                    if name in own:
+                        pieces_of_round.setdefault(k + rnd, []).append(own[name])
+            for stage, lag in ORDER:
+                if stage == "s": at(scores, k - lag)
+                if stage == "r": at(rowmax, k - lag)
+                if stage == "e": at(exponential, k - lag)
+                if stage == "t": at(transposes, k - lag)
+                if stage == "c": at(out_of_psum, k - lag)
+                if stage == "q": after_last_head(quantise, k - lag)
+                if stage == "p": run_pieces(k)
+                if stage == "v": after_last_head(weighted_values, k - lag)
+                if stage == "n": after_last_head(normalise_and_store, k - lag)

@@ -17,17 +17,33 @@ P = 128
 PACK = 4
 K_PASS = P * PACK
 Q_TILES = S // P
-TILES_PER_PASS = K_PASS // P
+BLOCKS = K_PASS // P
 E_PASSES = E // K_PASS
 KEY_PASSES = S // K_PASS
 HEADS_PER_GROUP = H // G
 SCALE = 1.0 / math.sqrt(D)
 MASKED = -(2.0**100)
-PV_LAG = 16
+HALF = P // 2
 
-ORDER = [('s', 0), ('v', 15), ('t', 3), ('n', 17), ('r', 0), ('c', 3), ('e', 1), ('q', 7), ('p', 0)]
-PLAN = [('x0', 0), ('x1', 1), ('x2', 2), ('x3', 3), ('q2', 4), ('v0', 5), ('v1', 6), ('x4', 7), ('x5', 8), ('x6', 9), ('x7', 10), ('v2', 12), ('v3', 13), ('q1', 14), ('q0', 19), ('K0', 24), ('Q3', 26), ('K1', 28)]
 FLOPS = 2 * B * G * S * E * D + 2 * 2 * B * H * D * (K_PASS * K_PASS + K_PASS * S)
+
+MEMORY = (3, 2, 0, 1, 4, 5, 6, 7)
+Q_ORDER = (7, 6, 5, 1, 4, 0, 3, 2)
+X_RUNS = (
+    ((384, slice(0, 32)), (256, slice(32, 64)), (0, slice(64, 128))),
+    ((512, slice(0, 128)),),
+)
+UNITS = (
+    (2, ((7, 0, 8, 0),)),
+    (2, ((6, 0, 7, 0),)),
+    (2, ((5, 0, 6, 0), (1, 6, 8, 4))),
+    (2, ((4, 0, 5, 0), (0, 6, 7, 4))),
+    (1, ((3, 0, 4, 0),)),
+    (1, ((2, 1, 4, 0),)),
+)
+STEPS_PER_BATCH = len(UNITS) * H
+ORDER = [("s",0),("v",15),("t",4),("n",16),("r",0),("e",2),("c",4),("q",7),("p",0)]
+PLAN = [("x0",2),("x1",3),("x2",4),("x3",5),("q1",6),("v0",7),("v1",8),("x4",9),("x5",10),("q2",10),("x6",11),("x7",12),("v2",14),("q3",14),("v3",15),("K0",17),("Q0",19),("K1",21)]
 
 
 def tile_multiheadattention_pa_t_kernel(tc, q, kg, x, Wv, bv, out):
@@ -36,12 +52,66 @@ def tile_multiheadattention_pa_t_kernel(tc, q, kg, x, Wv, bv, out):
         consts = ctx.enter_context(tc.tile_pool(name="consts", bufs=1))
         batch = ctx.enter_context(tc.tile_pool(name="batch", bufs=2))
         work = ctx.enter_context(tc.tile_pool(name="work", bufs=3))
+        prep = ctx.enter_context(tc.tile_pool(name="prep", bufs=2))
         ring = ctx.enter_context(tc.tile_pool(name="ring", bufs=4))
         wide = ctx.enter_context(tc.tile_pool(name="wide", bufs=3))
         small = ctx.enter_context(tc.tile_pool(name="small", bufs=6))
         psum_s = ctx.enter_context(tc.psum_pool(name="psum_s", bufs=4))
         psum_t = ctx.enter_context(tc.psum_pool(name="psum_t", bufs=3))
         psum_o = ctx.enter_context(tc.psum_pool(name="psum_o", bufs=1))
+
+        tiles = [{} for b in range(B)]
+
+        def tiles_of(b):
+            t = tiles[b]
+            t["k"] = batch.tile([P, G * Q_TILES * D], BF16, name="k_sb")
+            t["q"] = batch.tile([P, H * Q_TILES * D], BF16, name="q_sb")
+            t["kT"] = batch.tile([P, G * S], BF16, name="kT")
+            t["qT"] = batch.tile([P, H * S], BF16, name="qT")
+            t["x"] = batch.tile([P, (S // P) * E], BF16, name="x_sb")
+            t["x_codes"] = batch.tile([P, (S // P) * E_PASSES * P], U32, name="x_codes", align_bytes=64)
+            t["x_scales"] = batch.tile([P, (S // P) * E_PASSES * P], U8, name="x_scales", align_bytes=64)
+            t["v_codes"] = batch.tile([P, KEY_PASSES * G * D], U32, name="v_codes", align_bytes=64)
+            t["v_scales"] = v_scales[b % 2]
+            t["half_codes"] = half_codes[b % 2]
+            t["half_scales"] = half_scales[b % 2]
+
+        def load_k(b, g):
+            width = Q_TILES * D
+            nc.sync.dma_start(
+                out=tiles[b]["k"][:, g * width : (g + 1) * width].rearrange("p (i d) -> p i d", d=D),
+                in_=kg[b, g].rearrange("(i p) d -> p i d", p=P),
+            )
+
+        def load_q(b, i):
+            width = H * D
+            place = Q_ORDER.index(i)
+            nc.sync.dma_start(
+                out=tiles[b]["q"][:, place * width : (place + 1) * width].rearrange("p (h d) -> p h d", d=D),
+                in_=q[b, :, i * P : (i + 1) * P, :].rearrange("h p d -> p h d"),
+            )
+
+        def load_x(b, c):
+            width = PACK * E
+            for first, parts in X_RUNS[c]:
+                count = parts.stop - parts.start
+                nc.sync.dma_start(
+                    out=tiles[b]["x"][parts, c * width : (c + 1) * width],
+                    in_=x[b, first : first + PACK * count, :].rearrange("(p t) k -> p (t k)", t=PACK),
+                )
+
+        def load_batch(b):
+            tiles_of(b)
+            load_k(b, 0)
+            load_q(b, Q_TILES - 1)
+            load_q(b, Q_TILES - 2)
+            load_k(b, 1)
+            load_x(b, 0)
+            for i in (5, 1):
+                load_q(b, i)
+            load_x(b, 1)
+            for i in (4, 0, 3, 2):
+                load_q(b, i)
 
         ident_f = consts.tile([P, P], F32, name="ident_f")
         make_identity(nc, ident_f[:])
@@ -61,59 +131,30 @@ def tile_multiheadattention_pa_t_kernel(tc, q, kg, x, Wv, bv, out):
         mask_bf = consts.tile([P, P], BF16, name="mask_bf")
         nc.vector.tensor_copy(out=mask_bf[:], in_=mask_f[:])
 
-        e_rows = consts.tile([P, TILES_PER_PASS * H * S], BF16, name="e_rows")
-        e_rows_view = e_rows[:].rearrange("p (r h k) -> p r h k", r=TILES_PER_PASS, h=H)
-        for r in range(TILES_PER_PASS - 1):
-            nc.vector.memset(e_rows_view[:, r, :, S - K_PASS + (r + 1) * P :], 0.0)
-
-        tiles = [{} for b in range(B)]
-
-        def load_heads(b):
-            t = tiles[b]
-            t["k"] = batch.tile([P, G * Q_TILES * D], BF16, name="k_sb")
-            t["q"] = batch.tile([P, H * Q_TILES * D], BF16, name="q_sb")
-            t["kT"] = batch.tile([P, G * S], BF16, name="kT")
-            t["qT"] = batch.tile([P, H * S], BF16, name="qT")
-
-        def load_k(b, g):
-            width = Q_TILES * D
-            nc.sync.dma_start(
-                out=tiles[b]["k"][:, g * width : (g + 1) * width].rearrange("p (i d) -> p i d", d=D),
-                in_=kg[b, g].rearrange("(i p) d -> p i d", p=P),
-            )
-
-        def load_q(b, i):
-            width = H * D
-            nc.sync.dma_start(
-                out=tiles[b]["q"][:, i * width : (i + 1) * width].rearrange("p (h d) -> p h d", d=D),
-                in_=q[b, :, i * P : (i + 1) * P, :].rearrange("h p d -> p h d"),
-            )
-
-        def load_x(b):
-            t = tiles[b]
-            t["x"] = batch.tile([P, (S // P) * E], BF16, name="x_sb")
-            rows = 2 * P
-            for a in range(S // rows):
-                nc.sync.dma_start(
-                    out=t["x"][:, a * 2 * E : (a + 1) * 2 * E],
-                    in_=x[b, a * rows : (a + 1) * rows, :].rearrange("(p e) k -> p (e k)", e=2),
-                )
-            t["x_codes"] = batch.tile([P, (S // P) * E_PASSES * P], U32, name="x_codes", align_bytes=64)
-            t["x_scales"] = batch.tile([P, (S // P) * E_PASSES * P], U8, name="x_scales", align_bytes=64)
-            t["v_codes"] = batch.tile([P, G * KEY_PASSES * D], U32, name="v_codes", align_bytes=64)
-            t["v_scales"] = batch.tile([P, G * KEY_PASSES * D], U8, name="v_scales", align_bytes=64)
-
-        def load_batch(b):
-            load_heads(b)
-            load_k(b, 0)
-            load_q(b, Q_TILES - 1)
-            load_q(b, Q_TILES - 2)
-            load_k(b, 1)
-            load_x(b)
-            for i in reversed(range(Q_TILES - 2)):
-                load_q(b, i)
+        v_scales, half_codes, half_scales = [], [], []
+        for n in range(2):
+            scales = consts.tile([P, KEY_PASSES * G * D], U8, name="v_scales%d" % n, align_bytes=64)
+            codes_h = consts.tile([P, KEY_PASSES * G * D], U32, name="half_codes%d" % n, align_bytes=64)
+            scales_h = consts.tile([P, KEY_PASSES * G * D], U8, name="half_scales%d" % n, align_bytes=64)
+            nc.gpsimd.memset(scales[:].bitcast(U32), 0)
+            nc.gpsimd.memset(codes_h[:], 0)
+            nc.gpsimd.memset(scales_h[:].bitcast(U32), 0)
+            v_scales.append(scales)
+            half_codes.append(codes_h)
+            half_scales.append(scales_h)
 
         load_batch(0)
+
+        e_rows = []
+        for u, (passes, parts) in enumerate(UNITS):
+            rows = consts.tile([P, H, passes * K_PASS], BF16, name="e_rows%d" % u)
+            e_rows.append(rows)
+            covered = set()
+            for i, m0, m1, shift in parts:
+                covered.update(range(m0, m1))
+            for m in range(passes * BLOCKS):
+                if m not in covered:
+                    nc.vector.memset(rows[:, :, m * P : (m + 1) * P], 0.0)
 
         w_raw = consts.tile([P, G * E_PASSES * 2, 2 * D], BF16, name="w_raw")
         nc.scalar.dma_start(
@@ -140,11 +181,11 @@ def tile_multiheadattention_pa_t_kernel(tc, q, kg, x, Wv, bv, out):
             in_=w_grp[:].rearrange("p a d t -> p (a d t)"),
         )
 
-
         def x_piece(t, j):
             held = {}
             x_words = t["x"][:].bitcast(F32)
             words = E // 2
+            width = E_PASSES * K_PASS
 
             def on_tensor():
                 held["ps"] = psum_t.tile([P, E_PASSES * 2, P], F32, name="xt_ps", tag="t")
@@ -156,29 +197,33 @@ def tile_multiheadattention_pa_t_kernel(tc, q, kg, x, Wv, bv, out):
                     )
 
             def out_of_psum():
-                held["grp"] = work.tile([P, E_PASSES * K_PASS], BF16, name="x_grp", align_bytes=64)
+                if j % 2 == 0:
+                    t["x_grp"] = prep.tile([P, 2 * width], BF16, name="x_grp", align_bytes=64)
                 nc.scalar.copy(
-                    out=held["grp"][:].bitcast(F32).rearrange("p (c s u) -> p c s u", c=E_PASSES, u=2),
+                    out=t["x_grp"][:]
+                    .bitcast(F32)[:, (j % 2) * width // 2 : (j % 2 + 1) * width // 2]
+                    .rearrange("p (c s u) -> p c s u", c=E_PASSES, u=2),
                     in_=held["ps"][:].rearrange("p (c u) s -> p c s u", u=2),
                 )
+                held["grp"] = t["x_grp"]
 
             def quantise():
-                cols = slice(j * E_PASSES * P, (j + 1) * E_PASSES * P)
+                cols = slice((j - 1) * E_PASSES * P, (j + 1) * E_PASSES * P)
                 nc.vector.quantize_mx(
                     out=t["x_codes"][:, cols].bitcast(FP8X4),
                     scales=t["x_scales"][:, cols],
                     in_=held["grp"][:],
                 )
 
-            return on_tensor, out_of_psum, quantise
+            return on_tensor, out_of_psum, quantise if j % 2 == 1 else None, None
 
         def v_piece(t, kp, g):
             held = {}
 
             def on_tensor():
-                held["ps"] = psum_t.tile([P, TILES_PER_PASS, D], F32, name="v_ps", tag="t")
-                for tt in range(TILES_PER_PASS):
-                    j = kp * TILES_PER_PASS + tt
+                held["ps"] = psum_t.tile([P, PACK, D], F32, name="v_ps", tag="t")
+                for tt in range(PACK):
+                    j = kp * PACK + tt
                     for c in range(E_PASSES):
                         x_cols = slice((j * E_PASSES + c) * P, (j * E_PASSES + c + 1) * P)
                         w_cols = slice((c * G + g) * D, (c * G + g + 1) * D)
@@ -193,32 +238,44 @@ def tile_multiheadattention_pa_t_kernel(tc, q, kg, x, Wv, bv, out):
                         )
 
             def out_of_psum():
-                held["grp"] = work.tile([P, D * PACK], BF16, name="v_grp", align_bytes=64)
+                if g == 0:
+                    t["v_grp"] = prep.tile([P, G * D * PACK], BF16, name="v_grp", align_bytes=64)
                 nc.vector.tensor_tensor(
-                    out=held["grp"][:].rearrange("p (d t) -> p d t", t=PACK),
+                    out=t["v_grp"][:, g * D * PACK : (g + 1) * D * PACK].rearrange("p (d t) -> p d t", t=PACK),
                     in0=held["ps"][:].rearrange("p t d -> p d t"),
                     in1=bv_all[:, g * D : (g + 1) * D].unsqueeze(2).to_broadcast([P, D, PACK]),
                     op=ALU.add,
                 )
+                held["grp"] = t["v_grp"]
+
+            cols = slice(kp * G * D, (kp + 1) * G * D)
 
             def quantise():
-                cols = slice((g * KEY_PASSES + kp) * D, (g * KEY_PASSES + kp + 1) * D)
                 nc.vector.quantize_mx(
                     out=t["v_codes"][:, cols].bitcast(FP8X4),
                     scales=t["v_scales"][:, cols],
                     in_=held["grp"][:],
                 )
 
-            return on_tensor, out_of_psum, quantise
+            def halve():
+                rows = slice(HALF, P) if kp == 0 else slice(0, HALF)
+                nc.gpsimd.tensor_copy(out=t["half_codes"][rows, cols], in_=t["v_codes"][rows, cols])
+                nc.gpsimd.tensor_copy(
+                    out=t["half_scales"][rows, cols].bitcast(U32), in_=t["v_scales"][rows, cols].bitcast(U32)
+                )
 
-        def head_piece(rows, transposed, n):
+            if g < G - 1:
+                return on_tensor, out_of_psum, None, None
+            return on_tensor, out_of_psum, quantise, halve
+
+        def head_piece(rows, transposed, n, places):
             held = {}
 
             def on_tensor():
                 held["ps"] = psum_t.tile([P, S], BF16, name="hT_ps", tag="t")
                 for i in range(Q_TILES):
                     nc.tensor.transpose(
-                        held["ps"][:, i * P : (i + 1) * P],
+                        held["ps"][:, places[i] * P : (places[i] + 1) * P],
                         rows[:, (n * Q_TILES + i) * D : (n * Q_TILES + i + 1) * D],
                         ident_bf[:],
                     )
@@ -228,177 +285,191 @@ def tile_multiheadattention_pa_t_kernel(tc, q, kg, x, Wv, bv, out):
                     out=transposed[:, n * S : (n + 1) * S].bitcast(F32), in_=held["ps"][:].bitcast(F32)
                 )
 
-            return on_tensor, out_of_psum, None
-
-        def value_pieces(t):
-            pieces = [x_piece(t, j) for j in range(S // P)]
-            pieces += [v_piece(t, kp, g) for kp in range(KEY_PASSES) for g in range(G)]
-            return pieces
+            return on_tensor, out_of_psum, None, None
 
         def k_piece(t, g):
-            return head_piece(t["k"], t["kT"], g)
+            return head_piece(t["k"], t["kT"], g, [MEMORY.index(i) for i in range(Q_TILES)])
 
         def q_piece(t, n):
-            return head_piece(t["q"], t["qT"], n)
+            return head_piece(t["q"], t["qT"], n, range(Q_TILES))
 
-        steps_per_batch = Q_TILES * H
         pieces_of_round = {}
 
         def run_pieces(k):
-            for on_tensor, out_of_psum, quantise in pieces_of_round.get(k, []):
-                on_tensor()
-                out_of_psum()
-            for on_tensor, out_of_psum, quantise in pieces_of_round.get(k - 1, []):
-                if quantise is not None:
-                    quantise()
+            for piece in pieces_of_round.get(k, []):
+                piece[0]()
+                piece[1]()
+            for piece in pieces_of_round.get(k - 1, []):
+                if piece[2] is not None:
+                    piece[2]()
+            for piece in pieces_of_round.get(k - 3, []):
+                if piece[3] is not None:
+                    piece[3]()
 
-        ctx.enter_context(tc.manual_schedule())
-        for on_tensor, out_of_psum, quantise in (k_piece(tiles[0], 0), q_piece(tiles[0], 3)):
-            on_tensor()
-            out_of_psum()
-        pieces_of_round[0] = [k_piece(tiles[0], 1)]
-
-        steps = [(b, i, h) for b in range(B) for i in reversed(range(Q_TILES)) for h in range(H)]
+        steps = [(b, u, h) for b in range(B) for u in range(len(UNITS)) for h in range(H)]
         state = [{} for step in steps]
         shared = {}
 
-        def shape_of(i):
-            return i // TILES_PER_PASS + 1, i % TILES_PER_PASS
-
-        def width_of(i, c):
-            passes, r = shape_of(i)
-            return K_PASS if c < passes - 1 else (r + 1) * P
-
         def scores(n):
-            b, i, h = steps[n]
-            passes, r = shape_of(i)
+            b, u, h = steps[n]
+            passes, parts = UNITS[u]
             g = h // HEADS_PER_GROUP
-            q_cols = tiles[b]["qT"][:, (i * H + h) * P : (i * H + h + 1) * P]
             kT = tiles[b]["kT"]
             state[n]["s"] = []
             for c in range(passes):
                 s_ps = psum_s.tile([P, K_PASS], F32, name="s_ps", tag="s")
                 state[n]["s"].append(s_ps)
-                key0 = g * S + c * K_PASS
-                below = width_of(i, c) if c < passes - 1 else r * P
-                if below > 0:
-                    nc.tensor.matmul(
-                        s_ps[:, :below], lhsT=q_cols, rhs=kT[:, key0 : key0 + below], start=True, stop=True
-                    )
-                if c == passes - 1:
-                    block = slice(below, below + P)
-                    nc.tensor.matmul(
-                        s_ps[:, block],
-                        lhsT=q_cols,
-                        rhs=kT[:, key0 + below : key0 + below + P],
-                        start=True,
-                        stop=False,
-                    )
-                    nc.tensor.matmul(s_ps[:, block], lhsT=ident_bf[:], rhs=mask_bf[:], start=False, stop=True)
+                for i, m0, m1, shift in parts:
+                    place = Q_ORDER.index(i) * H + h
+                    q_cols = tiles[b]["qT"][:, place * P : (place + 1) * P]
+                    lo, hi = max(m0, c * BLOCKS), min(m1, (c + 1) * BLOCKS)
+                    diagonal = MEMORY.index(i) + shift
+                    if lo <= diagonal < hi:
+                        runs = ((lo, diagonal), (diagonal, diagonal + 1), (diagonal + 1, hi))
+                    else:
+                        runs = ((lo, hi),)
+                    for first, last in runs:
+                        if first >= last:
+                            continue
+                        cols = slice((first - c * BLOCKS) * P, (last - c * BLOCKS) * P)
+                        keys = slice(g * S + (first - shift) * P, g * S + (last - shift) * P)
+                        masked = first == diagonal
+                        nc.tensor.matmul(s_ps[:, cols], lhsT=q_cols, rhs=kT[:, keys], start=True, stop=not masked)
+                        if masked:
+                            nc.tensor.matmul(s_ps[:, cols], lhsT=ident_bf[:], rhs=mask_bf[:], start=False, stop=True)
 
         def rowmax(n):
-            b, i, h = steps[n]
-            passes, r = shape_of(i)
-            lowest = small.tile([P, passes], F32, name="lowest")
+            b, u, h = steps[n]
+            passes, parts = UNITS[u]
             minus_s = ring.tile([P, passes * K_PASS], F32, name="minus_s")
-            for c in range(passes):
-                width = width_of(i, c)
-                nc.vector.tensor_scalar(
-                    out=minus_s[:, c * K_PASS : c * K_PASS + width],
-                    in0=state[n]["s"][c][:, :width],
-                    scalar1=-SCALE,
-                    scalar2=None,
-                    op0=ALU.mult,
-                    op1=ALU.min,
-                    accum_out=lowest[:, c : c + 1],
-                )
             state[n]["minus_s"] = minus_s
-            if passes == 1:
-                state[n]["shift"] = lowest[:, 0:1]
-            else:
-                shift = small.tile([P, 1], F32, name="shift")
-                nc.gpsimd.tensor_scalar(
-                    out=shift[:], in0=lowest[:, 0:1], scalar1=lowest[:, 1:2], scalar2=None, op0=ALU.min
-                )
-                state[n]["shift"] = shift[:]
+            state[n]["shift"] = []
+            for i, m0, m1, shift in parts:
+                ranges = []
+                for c in range(passes):
+                    lo, hi = max(m0, c * BLOCKS), min(m1, (c + 1) * BLOCKS)
+                    if lo < hi:
+                        ranges.append((c, lo, hi))
+                lowest = small.tile([P, 2], F32, name="lowest")
+                for column, (c, lo, hi) in enumerate(ranges):
+                    nc.vector.tensor_scalar(
+                        out=minus_s[:, lo * P : hi * P],
+                        in0=state[n]["s"][c][:, (lo - c * BLOCKS) * P : (hi - c * BLOCKS) * P],
+                        scalar1=-SCALE,
+                        scalar2=None,
+                        op0=ALU.mult,
+                        op1=ALU.min,
+                        accum_out=lowest[:, column : column + 1],
+                    )
+                if len(ranges) == 1:
+                    state[n]["shift"].append(lowest[:, 0:1])
+                else:
+                    joined = small.tile([P, 1], F32, name="joined")
+                    nc.gpsimd.tensor_scalar(
+                        out=joined[:], in0=lowest[:, 0:1], scalar1=lowest[:, 1:2], scalar2=None, op0=ALU.min
+                    )
+                    state[n]["shift"].append(joined[:])
 
         def exponential(n):
-            b, i, h = steps[n]
-            passes, r = shape_of(i)
+            b, u, h = steps[n]
+            passes, parts = UNITS[u]
             if h == 0:
-                shared[(b, i)] = {"sums": small.tile([P, H], F32, name="sums")}
-            first = (r * H + h + 1) * S - passes * K_PASS
-            width = (i + 1) * P
-            nc.scalar.activation(
-                out=e_rows[:, first : first + width],
-                in_=state[n]["minus_s"][:, :width],
-                func=ACT.Exp,
-                bias=state[n]["shift"],
-                scale=-1.0,
-                accum_out=shared[(b, i)]["sums"][:, h : h + 1],
-            )
-            state[n]["e_words"] = e_rows[:].bitcast(F32)[:, first // 2 : first // 2 + passes * K_PASS // 2]
+                shared[(b, u)] = {"sums": small.tile([P, len(parts) * H], F32, name="sums")}
+            for part, (i, m0, m1, shift) in enumerate(parts):
+                nc.scalar.activation(
+                    out=e_rows[u][:, h, m0 * P : m1 * P],
+                    in_=state[n]["minus_s"][:, m0 * P : m1 * P],
+                    func=ACT.Exp,
+                    bias=state[n]["shift"][part],
+                    scale=-1.0,
+                    accum_out=shared[(b, u)]["sums"][:, part * H + h : part * H + h + 1],
+                )
 
         def transposes(n):
-            b, i, h = steps[n]
-            passes, r = shape_of(i)
-            et_ps = psum_t.tile([P, passes * 2, P], F32, name="et_ps", tag="t")
-            for cu in range(passes * 2):
-                nc.tensor.transpose(et_ps[:, cu, :], state[n]["e_words"][:, cu * P : (cu + 1) * P], ident_f[:])
+            b, u, h = steps[n]
+            passes, parts = UNITS[u]
+            if passes == 2 or h % 2 == 0:
+                et_ps = psum_t.tile([P, 2 * 2, P], F32, name="et_ps", tag="t")
+            else:
+                et_ps = state[n - 1]["et_ps"]
             state[n]["et_ps"] = et_ps
+            e_words = e_rows[u][:, h, :].bitcast(F32)
+            for c in range(passes):
+                for w in range(2):
+                    slot = c * 2 + w if passes == 2 else (h % 2) * 2 + w
+                    nc.tensor.transpose(
+                        et_ps[:, slot, :], e_words[:, c * 2 * P + w : (c + 1) * 2 * P : 2], ident_f[:]
+                    )
 
         def out_of_psum(n):
-            b, i, h = steps[n]
-            passes, r = shape_of(i)
-            width = passes * K_PASS
+            b, u, h = steps[n]
+            passes, parts = UNITS[u]
             if h == 0:
-                shared[(b, i)]["e_grp"] = wide.tile([P, H * width], BF16, name="e_grp", align_bytes=64)
-            e_grp = shared[(b, i)]["e_grp"]
+                shared[(b, u)]["e_grp"] = wide.tile([P, H * passes * K_PASS], BF16, name="e_grp", align_bytes=64)
+            if passes == 1 and h % 2 == 0:
+                return
+            first = (h * passes - (1 if passes == 1 else 0)) * K_PASS // 2
             nc.scalar.copy(
-                out=e_grp[:].bitcast(F32)[:, h * width // 2 : (h + 1) * width // 2].rearrange(
-                    "p (c s u) -> p c s u", c=passes, u=2
-                ),
-                in_=state[n]["et_ps"][:].rearrange("p (c u) s -> p c s u", u=2),
+                out=shared[(b, u)]["e_grp"][:]
+                .bitcast(F32)[:, first : first + K_PASS]
+                .rearrange("p (c s w) -> p c s w", c=2, w=2),
+                in_=state[n]["et_ps"][:].rearrange("p (c w) s -> p c s w", w=2),
             )
 
-        def quantise(b, i):
-            passes, r = shape_of(i)
+        def quantise(b, u):
+            passes, parts = UNITS[u]
             e_codes = wide.tile([P, H * passes * P], U32, name="e_codes", align_bytes=64)
             e_scales = wide.tile([P, H * passes * P], U8, name="e_scales", align_bytes=64)
             nc.vector.quantize_mx(
-                out=e_codes[:].bitcast(FP8X4), scales=e_scales[:], in_=shared[(b, i)]["e_grp"][:]
+                out=e_codes[:].bitcast(FP8X4), scales=e_scales[:], in_=shared[(b, u)]["e_grp"][:]
             )
-            shared[(b, i)]["e_codes"] = e_codes
-            shared[(b, i)]["e_scales"] = e_scales
-            inverse = small.tile([P, H], F32, name="inverse")
-            nc.vector.reciprocal(out=inverse[:], in_=shared[(b, i)]["sums"][:])
-            shared[(b, i)]["inverse"] = inverse
+            shared[(b, u)]["e_codes"] = e_codes
+            shared[(b, u)]["e_scales"] = e_scales
+            inverse = small.tile([P, len(parts) * H], F32, name="inverse")
+            nc.vector.reciprocal(out=inverse[:], in_=shared[(b, u)]["sums"][:])
+            shared[(b, u)]["inverse"] = inverse
+            shared[(b, u)]["o_ps"] = {}
 
-        def weighted_values(b, i):
-            passes, r = shape_of(i)
+        def weighted_values(b, u, part):
+            passes, parts = UNITS[u]
+            if part >= len(parts):
+                return
+            t = tiles[b]
             o_ps = psum_o.tile([P, H * D], F32, name="o_ps", tag="o")
+            shared[(b, u)]["o_ps"][part] = o_ps
+            full = (t["v_codes"], t["v_scales"])
+            half = (t["half_codes"], t["half_scales"])
+            if part == 1:
+                uses = ((1, half, 0),)
+            elif len(parts) == 2:
+                uses = ((0, full, 0), (1, half, 1))
+            else:
+                uses = tuple((c, full, c) for c in range(passes))
             for h in range(H):
                 g = h // HEADS_PER_GROUP
-                for c in range(passes):
+                for place, (c, (codes, scales), kp) in enumerate(uses):
                     e_cols = slice((h * passes + c) * P, (h * passes + c + 1) * P)
-                    v_cols = slice((g * KEY_PASSES + c) * D, (g * KEY_PASSES + c + 1) * D)
+                    v_cols = slice((kp * G + g) * D, (kp * G + g + 1) * D)
                     nc.tensor.matmul_mx(
                         out=o_ps[:, h * D : (h + 1) * D],
-                        lhsT=shared[(b, i)]["e_codes"][:, e_cols].bitcast(FP8X4),
-                        lhsT_scale=shared[(b, i)]["e_scales"][:, e_cols],
-                        rhs=tiles[b]["v_codes"][:, v_cols].bitcast(FP8X4),
-                        rhs_scale=tiles[b]["v_scales"][:, v_cols],
-                        start=(c == 0),
-                        stop=(c == passes - 1),
+                        lhsT=shared[(b, u)]["e_codes"][:, e_cols].bitcast(FP8X4),
+                        lhsT_scale=shared[(b, u)]["e_scales"][:, e_cols],
+                        rhs=codes[:, v_cols].bitcast(FP8X4),
+                        rhs_scale=scales[:, v_cols],
+                        start=(place == 0),
+                        stop=(place == len(uses) - 1),
                     )
-            shared[(b, i)]["o_ps"] = o_ps
 
-        def normalise_and_store(b, i):
+        def normalise_and_store(b, u, part):
+            passes, parts = UNITS[u]
+            if part >= len(parts):
+                return
+            i = parts[part][0]
             o_sb = work.tile([P, H * D], F32, name="o_sb")
             nc.vector.tensor_tensor(
                 out=o_sb[:].rearrange("p (h d) -> p h d", h=H),
-                in0=shared[(b, i)]["o_ps"][:].rearrange("p (h d) -> p h d", h=H),
-                in1=shared[(b, i)]["inverse"][:].unsqueeze(2).to_broadcast([P, H, D]),
+                in0=shared[(b, u)]["o_ps"][part][:].rearrange("p (h d) -> p h d", h=H),
+                in1=shared[(b, u)]["inverse"][:, part * H : (part + 1) * H].unsqueeze(2).to_broadcast([P, H, D]),
                 op=ALU.mult,
             )
             nc.sync.dma_start(out=out[b, i * P : (i + 1) * P, :], in_=o_sb[:])
@@ -407,31 +478,48 @@ def tile_multiheadattention_pa_t_kernel(tc, q, kg, x, Wv, bv, out):
             if 0 <= n < len(steps):
                 stage(n)
 
-        def after_last_head(stage, n):
+        def after_last_head(stage, n, *more):
             if 0 <= n < len(steps) and steps[n][2] == H - 1:
-                stage(steps[n][0], steps[n][1])
+                stage(steps[n][0], steps[n][1], *more)
 
-        for k in range(len(steps) + PV_LAG + 1):
-            b_now = k // steps_per_batch
-            if k % steps_per_batch == 0 and b_now < B:
-                x0, x1, x2, x3, x4, x5, x6, x7, v00, v01, v10, v11 = value_pieces(tiles[b_now])
-                own = {"x0": x0, "x1": x1, "x2": x2, "x3": x3, "x4": x4, "x5": x5, "x6": x6, "x7": x7}
-                own.update({"v0": v00, "v1": v01, "v2": v10, "v3": v11})
-                own.update({"q2": q_piece(tiles[b_now], 2), "q1": q_piece(tiles[b_now], 1), "q0": q_piece(tiles[b_now], 0)})
+        ctx.enter_context(tc.manual_schedule())
+        for piece in (k_piece(tiles[0], 0), q_piece(tiles[0], 0)):
+            piece[0]()
+            piece[1]()
+        pieces_of_round[0] = [k_piece(tiles[0], 1)]
+
+        LAST = max(lag for stage, lag in ORDER) + 2
+        for k in range(len(steps) + LAST):
+            b_now = k // STEPS_PER_BATCH
+            if k % STEPS_PER_BATCH == 0 and b_now < B:
+                t = tiles[b_now]
+                own = {"x%d" % j: x_piece(t, j) for j in range(S // P)}
+                own.update({"v%d" % (kp * G + g): v_piece(t, kp, g) for kp in range(KEY_PASSES) for g in range(G)})
+                own.update({"q%d" % n: q_piece(t, n) for n in range(1, 4)})
                 if b_now + 1 < B:
                     load_batch(b_now + 1)
-                    nt = tiles[b_now + 1]
-                    own.update({"K0": k_piece(nt, 0), "Q3": q_piece(nt, 3), "K1": k_piece(nt, 1)})
+                    own.update({"K0": k_piece(tiles[b_now + 1], 0), "K1": k_piece(tiles[b_now + 1], 1), "Q0": q_piece(tiles[b_now + 1], 0)})
                 for name, rnd in PLAN:
                     if name in own:
                         pieces_of_round.setdefault(k + rnd, []).append(own[name])
             for stage, lag in ORDER:
-                if stage == "s": at(scores, k - lag)
-                if stage == "r": at(rowmax, k - lag)
-                if stage == "e": at(exponential, k - lag)
-                if stage == "t": at(transposes, k - lag)
-                if stage == "c": at(out_of_psum, k - lag)
-                if stage == "q": after_last_head(quantise, k - lag)
-                if stage == "p": run_pieces(k)
-                if stage == "v": after_last_head(weighted_values, k - lag)
-                if stage == "n": after_last_head(normalise_and_store, k - lag)
+                if stage == "s":
+                    at(scores, k - lag)
+                if stage == "r":
+                    at(rowmax, k - lag)
+                if stage == "e":
+                    at(exponential, k - lag)
+                if stage == "t":
+                    at(transposes, k - lag)
+                if stage == "c":
+                    at(out_of_psum, k - lag)
+                if stage == "q":
+                    after_last_head(quantise, k - lag)
+                if stage == "p":
+                    run_pieces(k)
+                if stage == "v":
+                    after_last_head(weighted_values, k - lag, 0)
+                    after_last_head(weighted_values, k - lag - 2, 1)
+                if stage == "n":
+                    after_last_head(normalise_and_store, k - lag, 0)
+                    after_last_head(normalise_and_store, k - lag - 2, 1)

@@ -42,7 +42,7 @@ UNITS = (
     (1, ((2, 1, 4, 0),)),
 )
 STEPS_PER_BATCH = len(UNITS) * H
-ORDER = [("s",0),("v",15),("t",4),("n",16),("r",0),("e",2),("c",4),("q",7),("p",0)]
+ORDER = [("s",0),("v",0),("t",4),("n",0),("r",0),("e",2),("c",4),("q",7),("p",0)]
 PLAN = [("x0",2),("x1",3),("x2",4),("x3",5),("q1",6),("v0",7),("v1",8),("x4",9),("x5",10),("q2",10),("x6",11),("x7",12),("v2",14),("q3",14),("v3",15),("K0",17),("Q0",19),("K1",21)]
 
 
@@ -147,14 +147,14 @@ def tile_multiheadattention_pa_t_kernel(tc, q, kg, x, Wv, bv, out):
 
         e_rows = []
         for u, (passes, parts) in enumerate(UNITS):
-            rows = consts.tile([P, H, passes * K_PASS], BF16, name="e_rows%d" % u)
+            rows = consts.tile([P, H, 2, passes * K_PASS // 2], BF16, name="e_rows%d" % u)
             e_rows.append(rows)
             covered = set()
             for i, m0, m1, shift in parts:
                 covered.update(range(m0, m1))
             for m in range(passes * BLOCKS):
                 if m not in covered:
-                    nc.vector.memset(rows[:, :, m * P : (m + 1) * P], 0.0)
+                    nc.vector.memset(rows[:, :, :, m * HALF : (m + 1) * HALF], 0.0)
 
         w_raw = consts.tile([P, G * E_PASSES * 2, 2 * D], BF16, name="w_raw")
         nc.scalar.dma_start(
@@ -341,7 +341,7 @@ def tile_multiheadattention_pa_t_kernel(tc, q, kg, x, Wv, bv, out):
         def rowmax(n):
             b, u, h = steps[n]
             passes, parts = UNITS[u]
-            minus_s = ring.tile([P, passes * K_PASS], F32, name="minus_s")
+            minus_s = ring.tile([P, 2, passes * K_PASS // 2], F32, name="minus_s")
             state[n]["minus_s"] = minus_s
             state[n]["shift"] = []
             for i, m0, m1, shift in parts:
@@ -353,8 +353,10 @@ def tile_multiheadattention_pa_t_kernel(tc, q, kg, x, Wv, bv, out):
                 lowest = small.tile([P, 2], F32, name="lowest")
                 for column, (c, lo, hi) in enumerate(ranges):
                     nc.vector.tensor_scalar(
-                        out=minus_s[:, lo * P : hi * P],
-                        in0=state[n]["s"][c][:, (lo - c * BLOCKS) * P : (hi - c * BLOCKS) * P],
+                        out=minus_s[:, :, lo * HALF : hi * HALF].rearrange("p w (m e) -> p w m e", e=2),
+                        in0=state[n]["s"][c][:, (lo - c * BLOCKS) * P : (hi - c * BLOCKS) * P].rearrange(
+                            "p (m w e) -> p w m e", w=2, e=2
+                        ),
                         scalar1=-SCALE,
                         scalar2=None,
                         op0=ALU.mult,
@@ -377,8 +379,8 @@ def tile_multiheadattention_pa_t_kernel(tc, q, kg, x, Wv, bv, out):
                 shared[(b, u)] = {"sums": small.tile([P, len(parts) * H], F32, name="sums")}
             for part, (i, m0, m1, shift) in enumerate(parts):
                 nc.scalar.activation(
-                    out=e_rows[u][:, h, m0 * P : m1 * P],
-                    in_=state[n]["minus_s"][:, m0 * P : m1 * P],
+                    out=e_rows[u][:, h, :, m0 * HALF : m1 * HALF],
+                    in_=state[n]["minus_s"][:, :, m0 * HALF : m1 * HALF],
                     func=ACT.Exp,
                     bias=state[n]["shift"][part],
                     scale=-1.0,
@@ -393,13 +395,12 @@ def tile_multiheadattention_pa_t_kernel(tc, q, kg, x, Wv, bv, out):
             else:
                 et_ps = state[n - 1]["et_ps"]
             state[n]["et_ps"] = et_ps
-            e_words = e_rows[u][:, h, :].bitcast(F32)
+            e_words = e_rows[u][:, h, :, :].rearrange("p w k -> p (w k)").bitcast(F32)
             for c in range(passes):
                 for w in range(2):
                     slot = c * 2 + w if passes == 2 else (h % 2) * 2 + w
-                    nc.tensor.transpose(
-                        et_ps[:, slot, :], e_words[:, c * 2 * P + w : (c + 1) * 2 * P : 2], ident_f[:]
-                    )
+                    first = (w * passes + c) * P
+                    nc.tensor.transpose(et_ps[:, slot, :], e_words[:, first : first + P], ident_f[:])
 
         def out_of_psum(n):
             b, u, h = steps[n]
@@ -488,8 +489,13 @@ def tile_multiheadattention_pa_t_kernel(tc, q, kg, x, Wv, bv, out):
             piece[1]()
         pieces_of_round[0] = [k_piece(tiles[0], 1)]
 
-        LAST = max(lag for stage, lag in ORDER) + 2
-        for k in range(len(steps) + LAST):
+        waiting = []
+        done = {}
+        plan = dict(PLAN)
+        lags = dict(ORDER)
+        k = -1
+        while k < len(steps) + lags["q"] or waiting or done:
+            k += 1
             b_now = k // STEPS_PER_BATCH
             if k % STEPS_PER_BATCH == 0 and b_now < B:
                 t = tiles[b_now]
@@ -514,12 +520,17 @@ def tile_multiheadattention_pa_t_kernel(tc, q, kg, x, Wv, bv, out):
                 if stage == "c":
                     at(out_of_psum, k - lag)
                 if stage == "q":
-                    after_last_head(quantise, k - lag)
+                    n = k - lag
+                    after_last_head(quantise, n)
+                    if 0 <= n < len(steps) and steps[n][2] == H - 1:
+                        b, u, h = steps[n]
+                        for part in range(len(UNITS[u][1])):
+                            vg = b * STEPS_PER_BATCH + plan["v3"] + (4 if len(UNITS[u][1]) == 2 else 2)
+                            waiting.append((max(k + 1, vg), (b, u, part)))
                 if stage == "p":
                     run_pieces(k)
-                if stage == "v":
-                    after_last_head(weighted_values, k - lag, 0)
-                    after_last_head(weighted_values, k - lag - 2, 1)
-                if stage == "n":
-                    after_last_head(normalise_and_store, k - lag, 0)
-                    after_last_head(normalise_and_store, k - lag - 2, 1)
+                if stage == "v" and k % 2 == 0 and waiting and waiting[0][0] <= k:
+                    done[k + 1] = waiting.pop(0)[1]
+                    weighted_values(*done[k + 1])
+                if stage == "n" and k in done:
+                    normalise_and_store(*done.pop(k))

@@ -30,8 +30,8 @@ FLOPS = 2 * B * G * S * E * D + 2 * 2 * B * H * D * (K_PASS * K_PASS + K_PASS * 
 MEMORY = (3, 2, 0, 1, 4, 5, 6, 7)
 Q_ORDER = (7, 6, 5, 1, 4, 0, 3, 2)
 X_RUNS = (
-    ((384, slice(0, 32)), (256, slice(32, 64)), (0, slice(64, 128))),
-    ((512, slice(0, 128)),),
+    ((384, slice(0, 32), slice(0, 4)), (256, slice(32, 64), slice(0, 4)), (0, slice(64, 128), slice(0, 4))),
+    ((512, slice(0, 128), slice(0, 2)), (512, slice(0, 128), slice(2, 4))),
 )
 UNITS = (
     (2, ((7, 0, 8, 0),)),
@@ -51,7 +51,7 @@ def tile_multiheadattention_pa_t_kernel(tc, q, kg, x, Wv, bv, out):
     with ExitStack() as ctx:
         consts = ctx.enter_context(tc.tile_pool(name="consts", bufs=1))
         batch = ctx.enter_context(tc.tile_pool(name="batch", bufs=2))
-        work = ctx.enter_context(tc.tile_pool(name="work", bufs=3))
+        work = ctx.enter_context(tc.tile_pool(name="work", bufs=4))
         prep = ctx.enter_context(tc.tile_pool(name="prep", bufs=2))
         ring = ctx.enter_context(tc.tile_pool(name="ring", bufs=4))
         wide = ctx.enter_context(tc.tile_pool(name="wide", bufs=3))
@@ -91,27 +91,25 @@ def tile_multiheadattention_pa_t_kernel(tc, q, kg, x, Wv, bv, out):
                 in_=q[b, :, i * P : (i + 1) * P, :].rearrange("h p d -> p h d"),
             )
 
-        def load_x(b, c):
+        def load_x(b, c, n):
             width = PACK * E
-            for first, parts in X_RUNS[c]:
-                count = parts.stop - parts.start
-                nc.sync.dma_start(
-                    out=tiles[b]["x"][parts, c * width : (c + 1) * width],
-                    in_=x[b, first : first + PACK * count, :].rearrange("(p t) k -> p (t k)", t=PACK),
-                )
+            first, parts, slots = X_RUNS[c][n]
+            count = parts.stop - parts.start
+            nc.sync.dma_start(
+                out=tiles[b]["x"][parts, c * width + slots.start * E : c * width + slots.stop * E].rearrange(
+                    "p (t k) -> p t k", k=E
+                ),
+                in_=x[b, first : first + PACK * count, :].rearrange("(p t) k -> p t k", t=PACK)[:, slots, :],
+            )
 
-        def load_batch(b):
-            tiles_of(b)
-            load_k(b, 0)
-            load_q(b, Q_TILES - 1)
-            load_q(b, Q_TILES - 2)
-            load_k(b, 1)
-            load_x(b, 0)
-            for i in (5, 1):
-                load_q(b, i)
-            load_x(b, 1)
-            for i in (4, 0, 3, 2):
-                load_q(b, i)
+        LOADS = [(load_k, 0), (load_q, 7), (load_q, 6), (load_k, 1)]
+        LOADS += [(load_x, 0, n) for n in range(len(X_RUNS[0]))]
+        LOADS += [(load_x, 1, n) for n in range(len(X_RUNS[1]))]
+        LOADS += [(load_q, i) for i in Q_ORDER[2:]]
+
+        def load(b, n):
+            LOADS[n][0](b, *LOADS[n][1:])
+
 
         ident_f = consts.tile([P, P], F32, name="ident_f")
         make_identity(nc, ident_f[:])
@@ -143,7 +141,9 @@ def tile_multiheadattention_pa_t_kernel(tc, q, kg, x, Wv, bv, out):
             half_codes.append(codes_h)
             half_scales.append(scales_h)
 
-        load_batch(0)
+        tiles_of(0)
+        for n in range(len(LOADS)):
+            load(0, n)
 
         e_rows = []
         for u, (passes, parts) in enumerate(UNITS):
@@ -466,7 +466,7 @@ def tile_multiheadattention_pa_t_kernel(tc, q, kg, x, Wv, bv, out):
             if part >= len(parts):
                 return
             i = parts[part][0]
-            o_sb = work.tile([P, H * D], F32, name="o_sb")
+            o_sb = work.tile([P, H * D], F32, name="o_sb", tag="o")
             nc.vector.tensor_tensor(
                 out=o_sb[:].rearrange("p (h d) -> p h d", h=H),
                 in0=shared[(b, u)]["o_ps"][part][:].rearrange("p (h d) -> p h d", h=H),
@@ -503,11 +503,13 @@ def tile_multiheadattention_pa_t_kernel(tc, q, kg, x, Wv, bv, out):
                 own.update({"v%d" % (kp * G + g): v_piece(t, kp, g) for kp in range(KEY_PASSES) for g in range(G)})
                 own.update({"q%d" % n: q_piece(t, n) for n in range(1, 4)})
                 if b_now + 1 < B:
-                    load_batch(b_now + 1)
+                    tiles_of(b_now + 1)
                     own.update({"K0": k_piece(tiles[b_now + 1], 0), "K1": k_piece(tiles[b_now + 1], 1), "Q0": q_piece(tiles[b_now + 1], 0)})
                 for name, rnd in PLAN:
                     if name in own:
                         pieces_of_round.setdefault(k + rnd, []).append(own[name])
+            if b_now + 1 < B and k % STEPS_PER_BATCH < len(LOADS):
+                load(b_now + 1, k % STEPS_PER_BATCH)
             for stage, lag in ORDER:
                 if stage == "s":
                     at(scores, k - lag)

@@ -42,7 +42,9 @@ UNITS = (
     (1, ((2, 1, 4, 0),)),
 )
 STEPS_PER_BATCH = len(UNITS) * H
-ORDER = [("s",0),("v",0),("t",4),("n",0),("r",0),("e",2),("c",4),("q",7),("p",0)]
+MARGIN = 3
+W_ROUND = 4
+ORDER = [("s",0),("v",0),("t",4),("n",0),("r",0),("e",2),("c",4),("q",6),("p",0)]
 PLAN = [("x0",2),("x1",3),("x2",4),("x3",5),("q1",6),("v0",7),("v1",8),("x4",9),("x5",10),("q2",10),("x6",11),("x7",12),("v2",14),("q3",14),("v3",15),("K0",17),("Q0",19),("K1",21)]
 
 
@@ -129,6 +131,10 @@ def tile_multiheadattention_pa_t_kernel(tc, q, kg, x, Wv, bv, out):
         mask_bf = consts.tile([P, P], BF16, name="mask_bf")
         nc.vector.tensor_copy(out=mask_bf[:], in_=mask_f[:])
 
+        warm_ps = psum_t.tile([P, K_PASS], F32, name="warm_ps", tag="t")
+        for n in range(14):
+            nc.tensor.matmul(warm_ps[:, :P], lhsT=ident_bf[:], rhs=ident_bf[:], start=True, stop=True)
+
         v_scales, half_codes, half_scales = [], [], []
         for n in range(2):
             scales = consts.tile([P, KEY_PASSES * G * D], U8, name="v_scales%d" % n, align_bytes=64)
@@ -140,10 +146,6 @@ def tile_multiheadattention_pa_t_kernel(tc, q, kg, x, Wv, bv, out):
             v_scales.append(scales)
             half_codes.append(codes_h)
             half_scales.append(scales_h)
-
-        tiles_of(0)
-        for n in range(len(LOADS)):
-            load(0, n)
 
         e_rows = []
         for u, (passes, parts) in enumerate(UNITS):
@@ -157,29 +159,49 @@ def tile_multiheadattention_pa_t_kernel(tc, q, kg, x, Wv, bv, out):
                     nc.vector.memset(rows[:, :, :, m * HALF : (m + 1) * HALF], 0.0)
 
         w_raw = consts.tile([P, G * E_PASSES * 2, 2 * D], BF16, name="w_raw")
-        nc.scalar.dma_start(
-            out=w_raw[:], in_=Wv.rearrange("g (a p e) d -> p (g a) (e d)", p=P, e=2)
-        )
+        w_grp = consts.tile([P, E_PASSES * G, D, PACK], BF16, name="w_grp", align_bytes=64)
+        w_codes = consts.tile([P, E_PASSES * G * D], U32, name="w_codes", align_bytes=64)
+        w_scales = consts.tile([P, E_PASSES * G * D], U8, name="w_scales", align_bytes=64)
+        bv_row = consts.tile([P, G * D], BF16, name="bv_row")
+        nc.gpsimd.memset(bv_row[:], 0.0)
+        ones = consts.tile([P, P], BF16, name="ones")
+        nc.gpsimd.memset(ones[:], 1.0)
         bv_all = consts.tile([P, G * D], BF16, name="bv_all")
-        nc.scalar.dma_start(out=bv_all[:], in_=bv.rearrange("g d -> (g d)").partition_broadcast(P))
+
+        def load_w(b):
+            nc.sync.dma_start(out=w_raw[:], in_=Wv.rearrange("g (a p e) d -> p (g a) (e d)", p=P, e=2))
+            nc.sync.dma_start(out=bv_row[0:1, :], in_=bv.rearrange("(o g) d -> o (g d)", o=1))
+
+        def spread_bv():
+            spread = psum_t.tile([P, K_PASS], F32, name="spread", tag="t")
+            nc.tensor.matmul(spread[:, : G * D], lhsT=ones[:], rhs=bv_row[:], start=True, stop=True)
+            nc.scalar.copy(out=bv_all[:], in_=spread[:, : G * D])
+
+        def group_w():
+            for c in range(E_PASSES):
+                for g in range(G):
+                    first = (g * E_PASSES + c) * 2
+                    nc.vector.tensor_copy(
+                        out=w_grp[:, c * G + g, :, :].rearrange("p d (u e) -> p d u e", u=2),
+                        in_=w_raw[:, first : first + 2, :].rearrange("p u (e d) -> p d u e", e=2),
+                    )
+
+        def quantise_w():
+            nc.vector.quantize_mx(
+                out=w_codes[:].bitcast(FP8X4),
+                scales=w_scales[:],
+                in_=w_grp[:].rearrange("p a d t -> p (a d t)"),
+            )
+
         warm = consts.tile([P, 1], F32, name="warm")
         nc.vector.memset(warm[:], 0.0)
         nc.scalar.activation(out=warm[:], in_=warm[:], func=ACT.Exp)
-        w_grp = consts.tile([P, E_PASSES * G, D, PACK], BF16, name="w_grp", align_bytes=64)
-        for c in range(E_PASSES):
-            for g in range(G):
-                first = (g * E_PASSES + c) * 2
-                nc.vector.tensor_copy(
-                    out=w_grp[:, c * G + g, :, :].rearrange("p d (u e) -> p d u e", u=2),
-                    in_=w_raw[:, first : first + 2, :].rearrange("p u (e d) -> p d u e", e=2),
-                )
-        w_codes = consts.tile([P, E_PASSES * G * D], U32, name="w_codes", align_bytes=64)
-        w_scales = consts.tile([P, E_PASSES * G * D], U8, name="w_scales", align_bytes=64)
-        nc.vector.quantize_mx(
-            out=w_codes[:].bitcast(FP8X4),
-            scales=w_scales[:],
-            in_=w_grp[:].rearrange("p a d t -> p (a d t)"),
-        )
+
+        tiles_of(0)
+        for n in range(len(LOADS)):
+            load(0, n)
+            if n == 3:
+                load_w(0)
 
         def x_piece(t, j):
             held = {}
@@ -417,27 +439,29 @@ def tile_multiheadattention_pa_t_kernel(tc, q, kg, x, Wv, bv, out):
                 in_=state[n]["et_ps"][:].rearrange("p (c w) s -> p c s w", w=2),
             )
 
-        def quantise(b, u):
+        def quantise(b, u, heads):
             passes, parts = UNITS[u]
-            e_codes = wide.tile([P, H * passes * P], U32, name="e_codes", align_bytes=64)
-            e_scales = wide.tile([P, H * passes * P], U8, name="e_scales", align_bytes=64)
+            if heads[0] == 0:
+                shared[(b, u)]["e_codes"] = wide.tile([P, H * passes * P], U32, name="e_codes", align_bytes=64)
+                shared[(b, u)]["e_scales"] = wide.tile([P, H * passes * P], U8, name="e_scales", align_bytes=64)
+                shared[(b, u)]["inverse"] = small.tile([P, len(parts) * H], F32, name="inverse")
+                shared[(b, u)]["o_ps"] = {}
+            cols = slice(heads[0] * passes * P, (heads[-1] + 1) * passes * P)
             nc.vector.quantize_mx(
-                out=e_codes[:].bitcast(FP8X4), scales=e_scales[:], in_=shared[(b, u)]["e_grp"][:]
+                out=shared[(b, u)]["e_codes"][:, cols].bitcast(FP8X4),
+                scales=shared[(b, u)]["e_scales"][:, cols],
+                in_=shared[(b, u)]["e_grp"][:, cols.start * PACK : cols.stop * PACK],
             )
-            shared[(b, u)]["e_codes"] = e_codes
-            shared[(b, u)]["e_scales"] = e_scales
-            inverse = small.tile([P, len(parts) * H], F32, name="inverse")
-            nc.vector.reciprocal(out=inverse[:], in_=shared[(b, u)]["sums"][:])
-            shared[(b, u)]["inverse"] = inverse
-            shared[(b, u)]["o_ps"] = {}
+            sums = slice(heads[0], heads[-1] + 1 + (len(parts) - 1) * H)
+            nc.vector.reciprocal(
+                out=shared[(b, u)]["inverse"][:, sums], in_=shared[(b, u)]["sums"][:, sums]
+            )
 
-        def weighted_values(b, u, part):
+        def weighted_values(b, u, part, heads):
             passes, parts = UNITS[u]
-            if part >= len(parts):
-                return
             t = tiles[b]
             o_ps = psum_o.tile([P, H * D], F32, name="o_ps", tag="o")
-            shared[(b, u)]["o_ps"][part] = o_ps
+            shared[(b, u)]["o_ps"][(part, heads)] = o_ps
             full = (t["v_codes"], t["v_scales"])
             half = (t["half_codes"], t["half_scales"])
             if part == 1:
@@ -446,7 +470,7 @@ def tile_multiheadattention_pa_t_kernel(tc, q, kg, x, Wv, bv, out):
                 uses = ((0, full, 0), (1, half, 1))
             else:
                 uses = tuple((c, full, c) for c in range(passes))
-            for h in range(H):
+            for h in heads:
                 g = h // HEADS_PER_GROUP
                 for place, (c, (codes, scales), kp) in enumerate(uses):
                     e_cols = slice((h * passes + c) * P, (h * passes + c + 1) * P)
@@ -461,27 +485,24 @@ def tile_multiheadattention_pa_t_kernel(tc, q, kg, x, Wv, bv, out):
                         stop=(place == len(uses) - 1),
                     )
 
-        def normalise_and_store(b, u, part):
+        def normalise_and_store(b, u, part, heads):
             passes, parts = UNITS[u]
-            if part >= len(parts):
-                return
             i = parts[part][0]
             o_sb = work.tile([P, H * D], F32, name="o_sb", tag="o")
+            count = len(heads)
+            cols = slice(heads[0] * D, (heads[-1] + 1) * D)
+            sums = slice(part * H + heads[0], part * H + heads[-1] + 1)
             nc.vector.tensor_tensor(
-                out=o_sb[:].rearrange("p (h d) -> p h d", h=H),
-                in0=shared[(b, u)]["o_ps"][part][:].rearrange("p (h d) -> p h d", h=H),
-                in1=shared[(b, u)]["inverse"][:, part * H : (part + 1) * H].unsqueeze(2).to_broadcast([P, H, D]),
+                out=o_sb[:, cols].rearrange("p (h d) -> p h d", h=count),
+                in0=shared[(b, u)]["o_ps"][(part, heads)][:, cols].rearrange("p (h d) -> p h d", h=count),
+                in1=shared[(b, u)]["inverse"][:, sums].unsqueeze(2).to_broadcast([P, count, D]),
                 op=ALU.mult,
             )
-            nc.sync.dma_start(out=out[b, i * P : (i + 1) * P, :], in_=o_sb[:])
+            nc.sync.dma_start(out=out[b, i * P : (i + 1) * P, cols], in_=o_sb[:, cols])
 
         def at(stage, n):
             if 0 <= n < len(steps):
                 stage(n)
-
-        def after_last_head(stage, n, *more):
-            if 0 <= n < len(steps) and steps[n][2] == H - 1:
-                stage(steps[n][0], steps[n][1], *more)
 
         ctx.enter_context(tc.manual_schedule())
         for piece in (k_piece(tiles[0], 0), q_piece(tiles[0], 0)):
@@ -510,6 +531,11 @@ def tile_multiheadattention_pa_t_kernel(tc, q, kg, x, Wv, bv, out):
                         pieces_of_round.setdefault(k + rnd, []).append(own[name])
             if b_now + 1 < B and k % STEPS_PER_BATCH < len(LOADS):
                 load(b_now + 1, k % STEPS_PER_BATCH)
+            if k == W_ROUND:
+                group_w()
+            if k == W_ROUND + 1:
+                quantise_w()
+                spread_bv()
             for stage, lag in ORDER:
                 if stage == "s":
                     at(scores, k - lag)
@@ -523,15 +549,19 @@ def tile_multiheadattention_pa_t_kernel(tc, q, kg, x, Wv, bv, out):
                     at(out_of_psum, k - lag)
                 if stage == "q":
                     n = k - lag
-                    after_last_head(quantise, n)
-                    if 0 <= n < len(steps) and steps[n][2] == H - 1:
+                    if 0 <= n < len(steps):
                         b, u, h = steps[n]
-                        for part in range(len(UNITS[u][1])):
-                            vg = b * STEPS_PER_BATCH + plan["v3"] + (4 if len(UNITS[u][1]) == 2 else 2)
-                            waiting.append((max(k + 1, vg), (b, u, part)))
+                        count = 2 if (b, u) == (B - 1, len(UNITS) - 1) else H
+                        if h % count == count - 1:
+                            heads = tuple(range(h + 1 - count, h + 1))
+                            quantise(b, u, heads)
+                            for part in range(len(UNITS[u][1])):
+                                made = plan["v3"] if UNITS[u][0] == 2 else plan["v1"]
+                                vg = b * STEPS_PER_BATCH + made + (4 if len(UNITS[u][1]) == 2 else 2)
+                                waiting.append((max(k + MARGIN, vg), (b, u, part, heads)))
                 if stage == "p":
                     run_pieces(k)
-                if stage == "v" and k % 2 == 0 and waiting and waiting[0][0] <= k:
+                if stage == "v" and (k % 2 == 0 or k >= len(steps)) and waiting and waiting[0][0] <= k:
                     done[k + 1] = waiting.pop(0)[1]
                     weighted_values(*done[k + 1])
                 if stage == "n" and k in done:

@@ -45,7 +45,7 @@ STEPS_PER_BATCH = len(UNITS) * H
 MARGIN = 3
 W_ROUND = 4
 ORDER = [("s",0),("v",0),("t",4),("n",0),("r",0),("e",2),("c",4),("q",6),("p",0)]
-PLAN = [("x0",2),("x1",3),("x2",4),("x3",5),("q1",6),("v0",7),("v1",8),("x4",9),("x5",10),("q2",10),("x6",11),("x7",12),("v2",14),("q3",14),("v3",15),("K0",17),("Q0",19),("K1",21)]
+PLAN = [("x0",3),("x1",4),("x2",5),("q1",5),("x3",6),("v0",8),("q2",8),("v1",9),("x4",9),("x5",10),("x6",11),("x7",12),("q3",12),("v2",14),("v3",15),("K0",17),("Q0",19),("K1",21)]
 
 
 def tile_multiheadattention_pa_t_kernel(tc, q, kg, x, Wv, bv, out):
@@ -55,12 +55,10 @@ def tile_multiheadattention_pa_t_kernel(tc, q, kg, x, Wv, bv, out):
         batch = ctx.enter_context(tc.tile_pool(name="batch", bufs=2))
         work = ctx.enter_context(tc.tile_pool(name="work", bufs=4))
         prep = ctx.enter_context(tc.tile_pool(name="prep", bufs=2))
-        ring = ctx.enter_context(tc.tile_pool(name="ring", bufs=4))
+        ring = ctx.enter_context(tc.tile_pool(name="ring", bufs=5))
         wide = ctx.enter_context(tc.tile_pool(name="wide", bufs=3))
         small = ctx.enter_context(tc.tile_pool(name="small", bufs=6))
-        psum_s = ctx.enter_context(tc.psum_pool(name="psum_s", bufs=4))
-        psum_t = ctx.enter_context(tc.psum_pool(name="psum_t", bufs=3))
-        psum_o = ctx.enter_context(tc.psum_pool(name="psum_o", bufs=1))
+        psum = ctx.enter_context(tc.psum_pool(name="psum", bufs=8))
 
         tiles = [{} for b in range(B)]
 
@@ -106,8 +104,9 @@ def tile_multiheadattention_pa_t_kernel(tc, q, kg, x, Wv, bv, out):
 
         LOADS = [(load_k, 0), (load_q, 7), (load_q, 6), (load_k, 1)]
         LOADS += [(load_x, 0, n) for n in range(len(X_RUNS[0]))]
+        LOADS += [(load_q, i) for i in Q_ORDER[2:4]]
         LOADS += [(load_x, 1, n) for n in range(len(X_RUNS[1]))]
-        LOADS += [(load_q, i) for i in Q_ORDER[2:]]
+        LOADS += [(load_q, i) for i in Q_ORDER[4:]]
 
         def load(b, n):
             LOADS[n][0](b, *LOADS[n][1:])
@@ -131,7 +130,9 @@ def tile_multiheadattention_pa_t_kernel(tc, q, kg, x, Wv, bv, out):
         mask_bf = consts.tile([P, P], BF16, name="mask_bf")
         nc.vector.tensor_copy(out=mask_bf[:], in_=mask_f[:])
 
-        warm_ps = psum_t.tile([P, K_PASS], F32, name="warm_ps", tag="t")
+        minus_one = consts.tile([P, 2 * H], F32, name="minus_one")
+        nc.gpsimd.memset(minus_one[:], -1.0)
+        warm_ps = psum.tile([P, K_PASS], F32, name="warm_ps", tag="bank")
         for n in range(14):
             nc.tensor.matmul(warm_ps[:, :P], lhsT=ident_bf[:], rhs=ident_bf[:], start=True, stop=True)
 
@@ -158,8 +159,9 @@ def tile_multiheadattention_pa_t_kernel(tc, q, kg, x, Wv, bv, out):
                 if m not in covered:
                     nc.vector.memset(rows[:, :, :, m * HALF : (m + 1) * HALF], 0.0)
 
-        w_raw = consts.tile([P, G * E_PASSES * 2, 2 * D], BF16, name="w_raw")
-        w_grp = consts.tile([P, E_PASSES * G, D, PACK], BF16, name="w_grp", align_bytes=64)
+        w_wide = wide.tile([P, 2 * E_PASSES * G * D * PACK], BF16, name="w_wide", tag="e_grp", align_bytes=64)
+        w_raw = w_wide[:, : E_PASSES * G * D * PACK].rearrange("p (a k) -> p a k", k=2 * D)
+        w_grp = w_wide[:, E_PASSES * G * D * PACK :].rearrange("p (a d t) -> p a d t", d=D, t=PACK)
         w_codes = consts.tile([P, E_PASSES * G * D], U32, name="w_codes", align_bytes=64)
         w_scales = consts.tile([P, E_PASSES * G * D], U8, name="w_scales", align_bytes=64)
         bv_row = consts.tile([P, G * D], BF16, name="bv_row")
@@ -169,11 +171,11 @@ def tile_multiheadattention_pa_t_kernel(tc, q, kg, x, Wv, bv, out):
         bv_all = consts.tile([P, G * D], BF16, name="bv_all")
 
         def load_w(b):
-            nc.sync.dma_start(out=w_raw[:], in_=Wv.rearrange("g (a p e) d -> p (g a) (e d)", p=P, e=2))
+            nc.sync.dma_start(out=w_raw, in_=Wv.rearrange("g (a p e) d -> p (g a) (e d)", p=P, e=2))
             nc.sync.dma_start(out=bv_row[0:1, :], in_=bv.rearrange("(o g) d -> o (g d)", o=1))
 
         def spread_bv():
-            spread = psum_t.tile([P, K_PASS], F32, name="spread", tag="t")
+            spread = psum.tile([P, K_PASS], F32, name="spread", tag="bank")
             nc.tensor.matmul(spread[:, : G * D], lhsT=ones[:], rhs=bv_row[:], start=True, stop=True)
             nc.scalar.copy(out=bv_all[:], in_=spread[:, : G * D])
 
@@ -190,7 +192,7 @@ def tile_multiheadattention_pa_t_kernel(tc, q, kg, x, Wv, bv, out):
             nc.vector.quantize_mx(
                 out=w_codes[:].bitcast(FP8X4),
                 scales=w_scales[:],
-                in_=w_grp[:].rearrange("p a d t -> p (a d t)"),
+                in_=w_wide[:, E_PASSES * G * D * PACK :],
             )
 
         warm = consts.tile([P, 1], F32, name="warm")
@@ -210,7 +212,7 @@ def tile_multiheadattention_pa_t_kernel(tc, q, kg, x, Wv, bv, out):
             width = E_PASSES * K_PASS
 
             def on_tensor():
-                held["ps"] = psum_t.tile([P, E_PASSES * 2, P], F32, name="xt_ps", tag="t")
+                held["ps"] = psum.tile([P, E_PASSES * 2, P], F32, name="xt_ps", tag="bank")
                 for cu in range(E_PASSES * 2):
                     nc.tensor.transpose(
                         held["ps"][:, cu, :],
@@ -243,7 +245,7 @@ def tile_multiheadattention_pa_t_kernel(tc, q, kg, x, Wv, bv, out):
             held = {}
 
             def on_tensor():
-                held["ps"] = psum_t.tile([P, PACK, D], F32, name="v_ps", tag="t")
+                held["ps"] = psum.tile([P, PACK, D], F32, name="v_ps", tag="bank")
                 for tt in range(PACK):
                     j = kp * PACK + tt
                     for c in range(E_PASSES):
@@ -294,7 +296,7 @@ def tile_multiheadattention_pa_t_kernel(tc, q, kg, x, Wv, bv, out):
             held = {}
 
             def on_tensor():
-                held["ps"] = psum_t.tile([P, S], BF16, name="hT_ps", tag="t")
+                held["ps"] = psum.tile([P, S], BF16, name="hT_ps", tag="bank")
                 for i in range(Q_TILES):
                     nc.tensor.transpose(
                         held["ps"][:, places[i] * P : (places[i] + 1) * P],
@@ -339,7 +341,7 @@ def tile_multiheadattention_pa_t_kernel(tc, q, kg, x, Wv, bv, out):
             kT = tiles[b]["kT"]
             state[n]["s"] = []
             for c in range(passes):
-                s_ps = psum_s.tile([P, K_PASS], F32, name="s_ps", tag="s")
+                s_ps = psum.tile([P, K_PASS], F32, name="s_ps", tag="bank")
                 state[n]["s"].append(s_ps)
                 for i, m0, m1, shift in parts:
                     place = Q_ORDER.index(i) * H + h
@@ -413,7 +415,7 @@ def tile_multiheadattention_pa_t_kernel(tc, q, kg, x, Wv, bv, out):
             b, u, h = steps[n]
             passes, parts = UNITS[u]
             if passes == 2 or h % 2 == 0:
-                et_ps = psum_t.tile([P, 2 * 2, P], F32, name="et_ps", tag="t")
+                et_ps = psum.tile([P, 2 * 2, P], F32, name="et_ps", tag="bank")
             else:
                 et_ps = state[n - 1]["et_ps"]
             state[n]["et_ps"] = et_ps
@@ -428,7 +430,7 @@ def tile_multiheadattention_pa_t_kernel(tc, q, kg, x, Wv, bv, out):
             b, u, h = steps[n]
             passes, parts = UNITS[u]
             if h == 0:
-                shared[(b, u)]["e_grp"] = wide.tile([P, H * passes * K_PASS], BF16, name="e_grp", align_bytes=64)
+                shared[(b, u)]["e_grp"] = wide.tile([P, H * passes * K_PASS], BF16, name="e_grp", tag="e_grp", align_bytes=64)
             if passes == 1 and h % 2 == 0:
                 return
             first = (h * passes - (1 if passes == 1 else 0)) * K_PASS // 2
@@ -453,14 +455,17 @@ def tile_multiheadattention_pa_t_kernel(tc, q, kg, x, Wv, bv, out):
                 in_=shared[(b, u)]["e_grp"][:, cols.start * PACK : cols.stop * PACK],
             )
             sums = slice(heads[0], heads[-1] + 1 + (len(parts) - 1) * H)
-            nc.vector.reciprocal(
-                out=shared[(b, u)]["inverse"][:, sums], in_=shared[(b, u)]["sums"][:, sums]
+            nc.gpsimd.tensor_tensor(
+                out=shared[(b, u)]["inverse"][:, sums],
+                in0=shared[(b, u)]["sums"][:, sums],
+                in1=minus_one[:, sums],
+                op=ALU.pow,
             )
 
         def weighted_values(b, u, part, heads):
             passes, parts = UNITS[u]
             t = tiles[b]
-            o_ps = psum_o.tile([P, H * D], F32, name="o_ps", tag="o")
+            o_ps = psum.tile([P, H * D], F32, name="o_ps", tag="bank")
             shared[(b, u)]["o_ps"][(part, heads)] = o_ps
             full = (t["v_codes"], t["v_scales"])
             half = (t["half_codes"], t["half_scales"])

@@ -27,25 +27,25 @@ HALF = P // 2
 
 FLOPS = 2 * B * G * S * E * D + 2 * 2 * B * H * D * (K_PASS * K_PASS + K_PASS * S)
 
-MEMORY = (3, 2, 0, 1, 4, 5, 6, 7)
-Q_ORDER = (7, 6, 5, 1, 4, 0, 3, 2)
+MEMORY = (3, 2, 1, 0, 4, 5, 6, 7)
+Q_ORDER = (7, 6, 0, 5, 1, 4, 2, 3)
 X_RUNS = (
-    ((384, slice(0, 32), slice(0, 4)), (256, slice(32, 64), slice(0, 4)), (0, slice(64, 128), slice(0, 4))),
+    tuple((P * MEMORY[m], slice(32 * m, 32 * (m + 1)), slice(0, 4)) for m in range(4)),
     ((512, slice(0, 128), slice(0, 2)), (512, slice(0, 128), slice(2, 4))),
 )
 UNITS = (
     (2, ((7, 0, 8, 0),)),
-    (2, ((6, 0, 7, 0),)),
+    (2, ((6, 0, 7, 0), (0, 7, 8, 4))),
     (2, ((5, 0, 6, 0), (1, 6, 8, 4))),
-    (2, ((4, 0, 5, 0), (0, 6, 7, 4))),
+    (2, ((4, 0, 5, 0), (2, 5, 8, 4))),
     (1, ((3, 0, 4, 0),)),
-    (1, ((2, 1, 4, 0),)),
 )
+PAIRS = 3
 STEPS_PER_BATCH = len(UNITS) * H
 MARGIN = 3
 W_ROUND = 4
 ORDER = [("s",0),("v",0),("t",4),("n",0),("r",0),("e",2),("c",4),("q",6),("p",0)]
-PLAN = [("x0",3),("x1",4),("x2",5),("q1",5),("x3",6),("v0",8),("q2",8),("v1",9),("x4",9),("x5",10),("x6",11),("x7",12),("q3",12),("v2",14),("v3",15),("K0",17),("Q0",19),("K1",21)]
+PLAN = [("x0",3),("x1",4),("x2",5),("q2",5),("x3",6),("x4",7),("v0",8),("x5",8),("v1",9),("x6",9),("q3",9),("x7",10),("v2",12),("v3",13),("K0",14),("Q0",16),("K1",17),("Q1",19)]
 
 
 def tile_multiheadattention_pa_t_kernel(tc, q, kg, x, Wv, bv, out):
@@ -55,8 +55,9 @@ def tile_multiheadattention_pa_t_kernel(tc, q, kg, x, Wv, bv, out):
         batch = ctx.enter_context(tc.tile_pool(name="batch", bufs=2))
         work = ctx.enter_context(tc.tile_pool(name="work", bufs=4))
         prep = ctx.enter_context(tc.tile_pool(name="prep", bufs=2))
-        ring = ctx.enter_context(tc.tile_pool(name="ring", bufs=5))
-        wide = ctx.enter_context(tc.tile_pool(name="wide", bufs=3))
+        ring = ctx.enter_context(tc.tile_pool(name="ring", bufs=6))
+        wide = ctx.enter_context(tc.tile_pool(name="wide", bufs=4))
+        rows = ctx.enter_context(tc.tile_pool(name="rows", bufs=5))
         small = ctx.enter_context(tc.tile_pool(name="small", bufs=6))
         psum = ctx.enter_context(tc.psum_pool(name="psum", bufs=8))
 
@@ -73,8 +74,6 @@ def tile_multiheadattention_pa_t_kernel(tc, q, kg, x, Wv, bv, out):
             t["x_scales"] = batch.tile([P, (S // P) * E_PASSES * P], U8, name="x_scales", align_bytes=64)
             t["v_codes"] = batch.tile([P, KEY_PASSES * G * D], U32, name="v_codes", align_bytes=64)
             t["v_scales"] = v_scales[b % 2]
-            t["half_codes"] = half_codes[b % 2]
-            t["half_scales"] = half_scales[b % 2]
 
         def load_k(b, g):
             width = Q_TILES * D
@@ -102,11 +101,11 @@ def tile_multiheadattention_pa_t_kernel(tc, q, kg, x, Wv, bv, out):
                 in_=x[b, first : first + PACK * count, :].rearrange("(p t) k -> p t k", t=PACK)[:, slots, :],
             )
 
-        LOADS = [(load_k, 0), (load_q, 7), (load_q, 6), (load_k, 1)]
+        LOADS = [(load_k, 0), (load_q, 7), (load_q, 6), (load_k, 1), (load_q, 0), (load_q, 5)]
         LOADS += [(load_x, 0, n) for n in range(len(X_RUNS[0]))]
-        LOADS += [(load_q, i) for i in Q_ORDER[2:4]]
+        LOADS += [(load_q, 1), (load_q, 4)]
         LOADS += [(load_x, 1, n) for n in range(len(X_RUNS[1]))]
-        LOADS += [(load_q, i) for i in Q_ORDER[4:]]
+        LOADS += [(load_q, 2), (load_q, 3)]
 
         def load(b, n):
             LOADS[n][0](b, *LOADS[n][1:])
@@ -136,28 +135,18 @@ def tile_multiheadattention_pa_t_kernel(tc, q, kg, x, Wv, bv, out):
         for n in range(14):
             nc.tensor.matmul(warm_ps[:, :P], lhsT=ident_bf[:], rhs=ident_bf[:], start=True, stop=True)
 
-        v_scales, half_codes, half_scales = [], [], []
+        v_scales = []
         for n in range(2):
             scales = consts.tile([P, KEY_PASSES * G * D], U8, name="v_scales%d" % n, align_bytes=64)
-            codes_h = consts.tile([P, KEY_PASSES * G * D], U32, name="half_codes%d" % n, align_bytes=64)
-            scales_h = consts.tile([P, KEY_PASSES * G * D], U8, name="half_scales%d" % n, align_bytes=64)
             nc.gpsimd.memset(scales[:].bitcast(U32), 0)
-            nc.gpsimd.memset(codes_h[:], 0)
-            nc.gpsimd.memset(scales_h[:].bitcast(U32), 0)
             v_scales.append(scales)
-            half_codes.append(codes_h)
-            half_scales.append(scales_h)
-
-        e_rows = []
-        for u, (passes, parts) in enumerate(UNITS):
-            rows = consts.tile([P, H, 2, passes * K_PASS // 2], BF16, name="e_rows%d" % u)
-            e_rows.append(rows)
-            covered = set()
-            for i, m0, m1, shift in parts:
-                covered.update(range(m0, m1))
-            for m in range(passes * BLOCKS):
-                if m not in covered:
-                    nc.vector.memset(rows[:, :, :, m * HALF : (m + 1) * HALF], 0.0)
+        part_codes, part_scales = {}, {}
+        for u in range(1, PAIRS + 1):
+            codes_u = consts.tile([P, KEY_PASSES * G * D], U32, name="part_codes%d" % u, align_bytes=64)
+            scales_u = consts.tile([P, KEY_PASSES * G * D], U8, name="part_scales%d" % u, align_bytes=64)
+            nc.gpsimd.memset(codes_u[:], 0)
+            nc.gpsimd.memset(scales_u[:].bitcast(U32), 0)
+            part_codes[u], part_scales[u] = codes_u, scales_u
 
         w_wide = wide.tile([P, 2 * E_PASSES * G * D * PACK], BF16, name="w_wide", tag="e_grp", align_bytes=64)
         w_raw = w_wide[:, : E_PASSES * G * D * PACK].rearrange("p (a k) -> p a k", k=2 * D)
@@ -202,7 +191,7 @@ def tile_multiheadattention_pa_t_kernel(tc, q, kg, x, Wv, bv, out):
         tiles_of(0)
         for n in range(len(LOADS)):
             load(0, n)
-            if n == 3:
+            if n == 5 + len(X_RUNS[0]):
                 load_w(0)
 
         def x_piece(t, j):
@@ -281,16 +270,23 @@ def tile_multiheadattention_pa_t_kernel(tc, q, kg, x, Wv, bv, out):
                     in_=held["grp"][:],
                 )
 
-            def halve():
-                rows = slice(HALF, P) if kp == 0 else slice(0, HALF)
-                nc.gpsimd.tensor_copy(out=t["half_codes"][rows, cols], in_=t["v_codes"][rows, cols])
-                nc.gpsimd.tensor_copy(
-                    out=t["half_scales"][rows, cols].bitcast(U32), in_=t["v_scales"][rows, cols].bitcast(U32)
-                )
+            def restrict(u):
+                bound = 32 * (UNITS[u][1][0][2] - BLOCKS)
+                if kp == 1:
+                    runs = (slice(0, bound),)
+                elif bound == 32:
+                    runs = (slice(32, HALF), slice(HALF, P))
+                else:
+                    runs = (slice(bound, P),)
+                for rows in runs:
+                    nc.gpsimd.tensor_copy(out=part_codes[u][rows, cols], in_=t["v_codes"][rows, cols])
+                    nc.gpsimd.tensor_copy(
+                        out=part_scales[u][rows, cols].bitcast(U32), in_=t["v_scales"][rows, cols].bitcast(U32)
+                    )
 
             if g < G - 1:
                 return on_tensor, out_of_psum, None, None
-            return on_tensor, out_of_psum, quantise, halve
+            return on_tensor, out_of_psum, quantise, restrict
 
         def head_piece(rows, transposed, n, places):
             held = {}
@@ -326,9 +322,10 @@ def tile_multiheadattention_pa_t_kernel(tc, q, kg, x, Wv, bv, out):
             for piece in pieces_of_round.get(k - 1, []):
                 if piece[2] is not None:
                     piece[2]()
-            for piece in pieces_of_round.get(k - 3, []):
-                if piece[3] is not None:
-                    piece[3]()
+            for u in range(1, PAIRS + 1):
+                for piece in pieces_of_round.get(k - 2 - u, []):
+                    if piece[3] is not None:
+                        piece[3](u)
 
         steps = [(b, u, h) for b in range(B) for u in range(len(UNITS)) for h in range(H)]
         state = [{} for step in steps]
@@ -401,9 +398,11 @@ def tile_multiheadattention_pa_t_kernel(tc, q, kg, x, Wv, bv, out):
             passes, parts = UNITS[u]
             if h == 0:
                 shared[(b, u)] = {"sums": small.tile([P, len(parts) * H], F32, name="sums")}
+            e_row = rows.tile([P, 2, passes * K_PASS // 2], BF16, name="e_row")
+            state[n]["e_row"] = e_row
             for part, (i, m0, m1, shift) in enumerate(parts):
                 nc.scalar.activation(
-                    out=e_rows[u][:, h, :, m0 * HALF : m1 * HALF],
+                    out=e_row[:, :, m0 * HALF : m1 * HALF],
                     in_=state[n]["minus_s"][:, :, m0 * HALF : m1 * HALF],
                     func=ACT.Exp,
                     bias=state[n]["shift"][part],
@@ -419,7 +418,7 @@ def tile_multiheadattention_pa_t_kernel(tc, q, kg, x, Wv, bv, out):
             else:
                 et_ps = state[n - 1]["et_ps"]
             state[n]["et_ps"] = et_ps
-            e_words = e_rows[u][:, h, :, :].rearrange("p w k -> p (w k)").bitcast(F32)
+            e_words = state[n]["e_row"][:].rearrange("p w k -> p (w k)").bitcast(F32)
             for c in range(passes):
                 for w in range(2):
                     slot = c * 2 + w if passes == 2 else (h % 2) * 2 + w
@@ -468,7 +467,7 @@ def tile_multiheadattention_pa_t_kernel(tc, q, kg, x, Wv, bv, out):
             o_ps = psum.tile([P, H * D], F32, name="o_ps", tag="bank")
             shared[(b, u)]["o_ps"][(part, heads)] = o_ps
             full = (t["v_codes"], t["v_scales"])
-            half = (t["half_codes"], t["half_scales"])
+            half = (part_codes.get(u), part_scales.get(u))
             if part == 1:
                 uses = ((1, half, 0),)
             elif len(parts) == 2:
@@ -514,6 +513,7 @@ def tile_multiheadattention_pa_t_kernel(tc, q, kg, x, Wv, bv, out):
             piece[0]()
             piece[1]()
         pieces_of_round[0] = [k_piece(tiles[0], 1)]
+        pieces_of_round[1] = [q_piece(tiles[0], 1)]
 
         waiting = []
         done = {}
@@ -527,10 +527,10 @@ def tile_multiheadattention_pa_t_kernel(tc, q, kg, x, Wv, bv, out):
                 t = tiles[b_now]
                 own = {"x%d" % j: x_piece(t, j) for j in range(S // P)}
                 own.update({"v%d" % (kp * G + g): v_piece(t, kp, g) for kp in range(KEY_PASSES) for g in range(G)})
-                own.update({"q%d" % n: q_piece(t, n) for n in range(1, 4)})
+                own.update({"q%d" % n: q_piece(t, n) for n in range(2, 4)})
                 if b_now + 1 < B:
                     tiles_of(b_now + 1)
-                    own.update({"K0": k_piece(tiles[b_now + 1], 0), "K1": k_piece(tiles[b_now + 1], 1), "Q0": q_piece(tiles[b_now + 1], 0)})
+                    own.update({"K0": k_piece(tiles[b_now + 1], 0), "K1": k_piece(tiles[b_now + 1], 1), "Q0": q_piece(tiles[b_now + 1], 0), "Q1": q_piece(tiles[b_now + 1], 1)})
                 for name, rnd in PLAN:
                     if name in own:
                         pieces_of_round.setdefault(k + rnd, []).append(own[name])
@@ -562,7 +562,7 @@ def tile_multiheadattention_pa_t_kernel(tc, q, kg, x, Wv, bv, out):
                             quantise(b, u, heads)
                             for part in range(len(UNITS[u][1])):
                                 made = plan["v3"] if UNITS[u][0] == 2 else plan["v1"]
-                                vg = b * STEPS_PER_BATCH + made + (4 if len(UNITS[u][1]) == 2 else 2)
+                                vg = b * STEPS_PER_BATCH + made + (4 + u if len(UNITS[u][1]) == 2 else 2)
                                 waiting.append((max(k + MARGIN, vg), (b, u, part, heads)))
                 if stage == "p":
                     run_pieces(k)

@@ -7,6 +7,7 @@ from concourse.masks import make_identity
 F32 = mybir.dt.float32
 BF16 = mybir.dt.bfloat16
 U32 = mybir.dt.uint32
+I32 = mybir.dt.int32
 U8 = mybir.dt.uint8
 FP8X4 = mybir.dt.float8_e4m3fn_x4
 ALU = mybir.AluOpType
@@ -45,7 +46,7 @@ STEPS_PER_BATCH = len(UNITS) * H
 MARGIN = 3
 W_ROUND = 4
 ORDER = [("s",0),("v",0),("t",4),("n",0),("r",0),("e",2),("c",4),("q",6),("p",0)]
-PLAN = [("x0",3),("x1",4),("x2",5),("q2",5),("x3",6),("x4",7),("v0",8),("x5",8),("v1",9),("x6",9),("q3",9),("x7",10),("v2",12),("v3",13),("K0",14),("Q0",16),("K1",17),("Q1",19)]
+PLAN = [("x0",3),("x1",4),("x2",5),("x3",6),("x4",7),("x5",8),("x6",9),("x7",10),("v0",8),("v1",9),("v2",12),("v3",13),("q2",5),("q3",9),("K0",14),("Q0",16),("K1",17),("Q1",19)]
 
 
 def tile_multiheadattention_pa_t_kernel(tc, q, kg, x, Wv, bv, out):
@@ -129,8 +130,6 @@ def tile_multiheadattention_pa_t_kernel(tc, q, kg, x, Wv, bv, out):
         mask_bf = consts.tile([P, P], BF16, name="mask_bf")
         nc.vector.tensor_copy(out=mask_bf[:], in_=mask_f[:])
 
-        minus_one = consts.tile([P, 2 * H], F32, name="minus_one")
-        nc.gpsimd.memset(minus_one[:], -1.0)
         warm_ps = psum.tile([P, K_PASS], F32, name="warm_ps", tag="bank")
         for n in range(14):
             nc.tensor.matmul(warm_ps[:, :P], lhsT=ident_bf[:], rhs=ident_bf[:], start=True, stop=True)
@@ -272,17 +271,13 @@ def tile_multiheadattention_pa_t_kernel(tc, q, kg, x, Wv, bv, out):
 
             def restrict(u):
                 bound = 32 * (UNITS[u][1][0][2] - BLOCKS)
-                if kp == 1:
-                    runs = (slice(0, bound),)
-                elif bound == 32:
-                    runs = (slice(32, HALF), slice(HALF, P))
-                else:
-                    runs = (slice(bound, P),)
-                for rows in runs:
-                    nc.gpsimd.tensor_copy(out=part_codes[u][rows, cols], in_=t["v_codes"][rows, cols])
-                    nc.gpsimd.tensor_copy(
-                        out=part_scales[u][rows, cols].bitcast(U32), in_=t["v_scales"][rows, cols].bitcast(U32)
-                    )
+                rows = slice(bound, P) if kp == 0 else slice(0, bound)
+                nc.sync.dma_start(
+                    out=part_codes[u][rows, cols].bitcast(I32), in_=t["v_codes"][rows, cols].bitcast(I32)
+                )
+                nc.sync.dma_start(
+                    out=part_scales[u][rows, cols].bitcast(I32), in_=t["v_scales"][rows, cols].bitcast(I32)
+                )
 
             if g < G - 1:
                 return on_tensor, out_of_psum, None, None
@@ -454,11 +449,8 @@ def tile_multiheadattention_pa_t_kernel(tc, q, kg, x, Wv, bv, out):
                 in_=shared[(b, u)]["e_grp"][:, cols.start * PACK : cols.stop * PACK],
             )
             sums = slice(heads[0], heads[-1] + 1 + (len(parts) - 1) * H)
-            nc.gpsimd.tensor_tensor(
-                out=shared[(b, u)]["inverse"][:, sums],
-                in0=shared[(b, u)]["sums"][:, sums],
-                in1=minus_one[:, sums],
-                op=ALU.pow,
+            nc.vector.reciprocal(
+                out=shared[(b, u)]["inverse"][:, sums], in_=shared[(b, u)]["sums"][:, sums]
             )
 
         def weighted_values(b, u, part, heads):

@@ -29,7 +29,6 @@ HALF = P // 2
 FLOPS = 2 * B * G * S * E * D + 2 * 2 * B * H * D * (K_PASS * K_PASS + K_PASS * S)
 
 MEMORY = (3, 2, 1, 0, 4, 5, 6, 7)
-Q_ORDER = (7, 6, 0, 5, 1, 4, 2, 3)
 X_RUNS = (
     tuple((P * MEMORY[m], slice(32 * m, 32 * (m + 1)), slice(0, 4)) for m in range(4)),
     ((512, slice(0, 128), slice(0, 2)), (512, slice(0, 128), slice(2, 4))),
@@ -42,11 +41,17 @@ UNITS = (
     (1, ((3, 0, 4, 0),)),
 )
 PAIRS = 3
+FIRST_ORDER = (4, 0, 1, 2, 3)
+ORDER_OF_UNITS = (FIRST_ORDER,) + ((0, 1, 2, 3, 4),) * (B - 1)
+Q_ORDER = tuple(tuple(part[0] for u in order for part in UNITS[u][1]) for order in ORDER_OF_UNITS)
 STEPS_PER_BATCH = len(UNITS) * H
 MARGIN = 3
-W_ROUND = 4
+ON_S = ((3, 3, 0), (3, 3, 1))
+W_ROUND = 6
 ORDER = [("s",0),("v",0),("t",4),("n",0),("r",0),("e",2),("c",4),("q",6),("p",0)]
 PLAN = [("x0",3),("x1",4),("x2",5),("x3",6),("x4",7),("x5",8),("x6",9),("x7",10),("v0",8),("v1",9),("v2",12),("v3",13),("q2",5),("q3",9),("K0",14),("Q0",16),("K1",17),("Q1",19)]
+PLAN0 = [("kA1",0),("qB",1),("kB0",2),("kB1",3),("x0",5),("x1",6),("x2",7),("x3",8),("x4",9),("x5",10),("x6",11),("x7",12),("v0",10),("v1",11),("v2",14),("v3",15),("q1",5),("q2",8),("q3",12),("K0",15),("Q0",17),("K1",18),("Q1",19)]
+NX = 4
 
 
 def tile_multiheadattention_pa_t_kernel(tc, q, kg, x, Wv, bv, out):
@@ -54,12 +59,12 @@ def tile_multiheadattention_pa_t_kernel(tc, q, kg, x, Wv, bv, out):
     with ExitStack() as ctx:
         consts = ctx.enter_context(tc.tile_pool(name="consts", bufs=1))
         batch = ctx.enter_context(tc.tile_pool(name="batch", bufs=2))
-        work = ctx.enter_context(tc.tile_pool(name="work", bufs=4))
+        work = ctx.enter_context(tc.tile_pool(name="work", bufs=6))
         prep = ctx.enter_context(tc.tile_pool(name="prep", bufs=2))
-        ring = ctx.enter_context(tc.tile_pool(name="ring", bufs=6))
+        ring = ctx.enter_context(tc.tile_pool(name="ring", bufs=8))
         wide = ctx.enter_context(tc.tile_pool(name="wide", bufs=4))
         rows = ctx.enter_context(tc.tile_pool(name="rows", bufs=5))
-        small = ctx.enter_context(tc.tile_pool(name="small", bufs=6))
+        small = ctx.enter_context(tc.tile_pool(name="small", bufs=24))
         psum = ctx.enter_context(tc.psum_pool(name="psum", bufs=8))
 
         tiles = [{} for b in range(B)]
@@ -76,16 +81,16 @@ def tile_multiheadattention_pa_t_kernel(tc, q, kg, x, Wv, bv, out):
             t["v_codes"] = batch.tile([P, KEY_PASSES * G * D], U32, name="v_codes", align_bytes=64)
             t["v_scales"] = v_scales[b % 2]
 
-        def load_k(b, g):
-            width = Q_TILES * D
+        def load_k(b, g, i0, i1):
+            first = g * Q_TILES
             nc.sync.dma_start(
-                out=tiles[b]["k"][:, g * width : (g + 1) * width].rearrange("p (i d) -> p i d", d=D),
-                in_=kg[b, g].rearrange("(i p) d -> p i d", p=P),
+                out=tiles[b]["k"][:, (first + i0) * D : (first + i1) * D].rearrange("p (i d) -> p i d", d=D),
+                in_=kg[b, g, i0 * P : i1 * P, :].rearrange("(i p) d -> p i d", p=P),
             )
 
-        def load_q(b, i):
+        def load_q(b, place):
             width = H * D
-            place = Q_ORDER.index(i)
+            i = Q_ORDER[b][place]
             nc.sync.dma_start(
                 out=tiles[b]["q"][:, place * width : (place + 1) * width].rearrange("p (h d) -> p h d", d=D),
                 in_=q[b, :, i * P : (i + 1) * P, :].rearrange("h p d -> p h d"),
@@ -102,14 +107,12 @@ def tile_multiheadattention_pa_t_kernel(tc, q, kg, x, Wv, bv, out):
                 in_=x[b, first : first + PACK * count, :].rearrange("(p t) k -> p t k", t=PACK)[:, slots, :],
             )
 
-        LOADS = [(load_k, 0), (load_q, 7), (load_q, 6), (load_k, 1), (load_q, 0), (load_q, 5)]
-        LOADS += [(load_x, 0, n) for n in range(len(X_RUNS[0]))]
-        LOADS += [(load_q, 1), (load_q, 4)]
-        LOADS += [(load_x, 1, n) for n in range(len(X_RUNS[1]))]
-        LOADS += [(load_q, 2), (load_q, 3)]
-
-        def load(b, n):
-            LOADS[n][0](b, *LOADS[n][1:])
+        LOADS = [(load_k, 0, 0, 8), (load_q, 0), (load_q, 1), (load_k, 1, 0, 8), (load_q, 2), (load_q, 3)]
+        FIRST_LOADS = [(load_k, 0, 0, 4), (load_q, 0), (load_k, 1, 0, 4), (load_q, 1), (load_k, 0, 4, 8), (load_k, 1, 4, 8)]
+        REST = [(load_x, 0, n) for n in range(len(X_RUNS[0]))]
+        REST_X1 = [(load_x, 1, n) for n in range(len(X_RUNS[1]))]
+        LOADS += REST + [(load_q, 4), (load_q, 5)] + REST_X1 + [(load_q, 6), (load_q, 7)]
+        FIRST_LOADS += REST[:NX] + [(load_q, 2), (load_q, 3)] + REST[NX:] + [(lambda b: load_w(b),)] + [(load_q, 4), (load_q, 5)] + REST_X1 + [(load_q, 6), (load_q, 7)]
 
 
         ident_f = consts.tile([P, P], F32, name="ident_f")
@@ -131,7 +134,7 @@ def tile_multiheadattention_pa_t_kernel(tc, q, kg, x, Wv, bv, out):
         nc.vector.tensor_copy(out=mask_bf[:], in_=mask_f[:])
 
         warm_ps = psum.tile([P, K_PASS], F32, name="warm_ps", tag="bank")
-        for n in range(14):
+        for n in range(10):
             nc.tensor.matmul(warm_ps[:, :P], lhsT=ident_bf[:], rhs=ident_bf[:], start=True, stop=True)
 
         v_scales = []
@@ -188,10 +191,8 @@ def tile_multiheadattention_pa_t_kernel(tc, q, kg, x, Wv, bv, out):
         nc.scalar.activation(out=warm[:], in_=warm[:], func=ACT.Exp)
 
         tiles_of(0)
-        for n in range(len(LOADS)):
-            load(0, n)
-            if n == 5 + len(X_RUNS[0]):
-                load_w(0)
+        for what, *where in FIRST_LOADS:
+            what(0, *where)
 
         def x_piece(t, j):
             held = {}
@@ -283,12 +284,12 @@ def tile_multiheadattention_pa_t_kernel(tc, q, kg, x, Wv, bv, out):
                 return on_tensor, out_of_psum, None, None
             return on_tensor, out_of_psum, quantise, restrict
 
-        def head_piece(rows, transposed, n, places):
+        def head_piece(rows, transposed, n, places, i0=0, i1=Q_TILES):
             held = {}
 
             def on_tensor():
                 held["ps"] = psum.tile([P, S], BF16, name="hT_ps", tag="bank")
-                for i in range(Q_TILES):
+                for i in range(i0, i1):
                     nc.tensor.transpose(
                         held["ps"][:, places[i] * P : (places[i] + 1) * P],
                         rows[:, (n * Q_TILES + i) * D : (n * Q_TILES + i + 1) * D],
@@ -297,16 +298,17 @@ def tile_multiheadattention_pa_t_kernel(tc, q, kg, x, Wv, bv, out):
 
             def out_of_psum():
                 nc.scalar.copy(
-                    out=transposed[:, n * S : (n + 1) * S].bitcast(F32), in_=held["ps"][:].bitcast(F32)
+                    out=transposed[:, n * S + i0 * P : n * S + i1 * P].bitcast(F32),
+                    in_=held["ps"][:, i0 * P : i1 * P].bitcast(F32),
                 )
 
             return on_tensor, out_of_psum, None, None
 
-        def k_piece(t, g):
-            return head_piece(t["k"], t["kT"], g, [MEMORY.index(i) for i in range(Q_TILES)])
+        def k_piece(t, g, *blocks):
+            return head_piece(t["k"], t["kT"], g, [MEMORY.index(i) for i in range(Q_TILES)], *blocks)
 
-        def q_piece(t, n):
-            return head_piece(t["q"], t["qT"], n, range(Q_TILES))
+        def q_piece(t, n, *rows):
+            return head_piece(t["q"], t["qT"], n, range(Q_TILES), *rows)
 
         pieces_of_round = {}
 
@@ -322,7 +324,7 @@ def tile_multiheadattention_pa_t_kernel(tc, q, kg, x, Wv, bv, out):
                     if piece[3] is not None:
                         piece[3](u)
 
-        steps = [(b, u, h) for b in range(B) for u in range(len(UNITS)) for h in range(H)]
+        steps = [(b, u, h) for b in range(B) for u in ORDER_OF_UNITS[b] for h in range(H)]
         state = [{} for step in steps]
         shared = {}
 
@@ -336,7 +338,7 @@ def tile_multiheadattention_pa_t_kernel(tc, q, kg, x, Wv, bv, out):
                 s_ps = psum.tile([P, K_PASS], F32, name="s_ps", tag="bank")
                 state[n]["s"].append(s_ps)
                 for i, m0, m1, shift in parts:
-                    place = Q_ORDER.index(i) * H + h
+                    place = Q_ORDER[b].index(i) * H + h
                     q_cols = tiles[b]["qT"][:, place * P : (place + 1) * P]
                     lo, hi = max(m0, c * BLOCKS), min(m1, (c + 1) * BLOCKS)
                     diagonal = MEMORY.index(i) + shift
@@ -481,6 +483,9 @@ def tile_multiheadattention_pa_t_kernel(tc, q, kg, x, Wv, bv, out):
                         stop=(place == len(uses) - 1),
                     )
 
+        def on_scalar(b, u, part):
+            return (b, u, part) in ON_S
+
         def normalise_and_store(b, u, part, heads):
             passes, parts = UNITS[u]
             i = parts[part][0]
@@ -488,12 +493,21 @@ def tile_multiheadattention_pa_t_kernel(tc, q, kg, x, Wv, bv, out):
             count = len(heads)
             cols = slice(heads[0] * D, (heads[-1] + 1) * D)
             sums = slice(part * H + heads[0], part * H + heads[-1] + 1)
-            nc.vector.tensor_tensor(
-                out=o_sb[:, cols].rearrange("p (h d) -> p h d", h=count),
-                in0=shared[(b, u)]["o_ps"][(part, heads)][:, cols].rearrange("p (h d) -> p h d", h=count),
-                in1=shared[(b, u)]["inverse"][:, sums].unsqueeze(2).to_broadcast([P, count, D]),
-                op=ALU.mult,
-            )
+            if on_scalar(b, u, part):
+                for h in heads:
+                    nc.scalar.activation(
+                        out=o_sb[:, h * D : (h + 1) * D],
+                        in_=shared[(b, u)]["o_ps"][(part, heads)][:, h * D : (h + 1) * D],
+                        func=ACT.Copy,
+                        scale=shared[(b, u)]["inverse"][:, part * H + h : part * H + h + 1],
+                    )
+            else:
+                nc.vector.tensor_tensor(
+                    out=o_sb[:, cols].rearrange("p (h d) -> p h d", h=count),
+                    in0=shared[(b, u)]["o_ps"][(part, heads)][:, cols].rearrange("p (h d) -> p h d", h=count),
+                    in1=shared[(b, u)]["inverse"][:, sums].unsqueeze(2).to_broadcast([P, count, D]),
+                    op=ALU.mult,
+                )
             nc.sync.dma_start(out=out[b, i * P : (i + 1) * P, cols], in_=o_sb[:, cols])
 
         def at(stage, n):
@@ -501,15 +515,12 @@ def tile_multiheadattention_pa_t_kernel(tc, q, kg, x, Wv, bv, out):
                 stage(n)
 
         ctx.enter_context(tc.manual_schedule())
-        for piece in (k_piece(tiles[0], 0), q_piece(tiles[0], 0)):
+        for piece in (k_piece(tiles[0], 0, 0, 4), q_piece(tiles[0], 0, 0, 4)):
             piece[0]()
             piece[1]()
-        pieces_of_round[0] = [k_piece(tiles[0], 1)]
-        pieces_of_round[1] = [q_piece(tiles[0], 1)]
 
         waiting = []
         done = {}
-        plan = dict(PLAN)
         lags = dict(ORDER)
         k = -1
         while k < len(steps) + lags["q"] or waiting or done:
@@ -519,15 +530,18 @@ def tile_multiheadattention_pa_t_kernel(tc, q, kg, x, Wv, bv, out):
                 t = tiles[b_now]
                 own = {"x%d" % j: x_piece(t, j) for j in range(S // P)}
                 own.update({"v%d" % (kp * G + g): v_piece(t, kp, g) for kp in range(KEY_PASSES) for g in range(G)})
-                own.update({"q%d" % n: q_piece(t, n) for n in range(2, 4)})
+                own.update({"q%d" % n: q_piece(t, n) for n in range(1 if b_now == 0 else 2, 4)})
+                if b_now == 0:
+                    own.update({"qB": q_piece(t, 0, 4, 8), "kA1": k_piece(t, 1, 0, 4), "kB0": k_piece(t, 0, 4, 8), "kB1": k_piece(t, 1, 4, 8)})
                 if b_now + 1 < B:
                     tiles_of(b_now + 1)
                     own.update({"K0": k_piece(tiles[b_now + 1], 0), "K1": k_piece(tiles[b_now + 1], 1), "Q0": q_piece(tiles[b_now + 1], 0), "Q1": q_piece(tiles[b_now + 1], 1)})
-                for name, rnd in PLAN:
+                for name, rnd in PLAN0 if b_now == 0 else PLAN:
                     if name in own:
                         pieces_of_round.setdefault(k + rnd, []).append(own[name])
             if b_now + 1 < B and k % STEPS_PER_BATCH < len(LOADS):
-                load(b_now + 1, k % STEPS_PER_BATCH)
+                what, *where = LOADS[k % STEPS_PER_BATCH]
+                what(b_now + 1, *where)
             if k == W_ROUND:
                 group_w()
             if k == W_ROUND + 1:
@@ -553,6 +567,7 @@ def tile_multiheadattention_pa_t_kernel(tc, q, kg, x, Wv, bv, out):
                             heads = tuple(range(h + 1 - count, h + 1))
                             quantise(b, u, heads)
                             for part in range(len(UNITS[u][1])):
+                                plan = dict(PLAN0 if b == 0 else PLAN)
                                 made = plan["v3"] if UNITS[u][0] == 2 else plan["v1"]
                                 vg = b * STEPS_PER_BATCH + made + (4 + u if len(UNITS[u][1]) == 2 else 2)
                                 waiting.append((max(k + MARGIN, vg), (b, u, part, heads)))
@@ -561,5 +576,7 @@ def tile_multiheadattention_pa_t_kernel(tc, q, kg, x, Wv, bv, out):
                 if stage == "v" and (k % 2 == 0 or k >= len(steps)) and waiting and waiting[0][0] <= k:
                     done[k + 1] = waiting.pop(0)[1]
                     weighted_values(*done[k + 1])
-                if stage == "n" and k in done:
+                if stage == "n" and k in done and not on_scalar(*done[k][:3]):
+                    normalise_and_store(*done.pop(k))
+                if stage == "p" and k in done:
                     normalise_and_store(*done.pop(k))

import math
from contextlib import ExitStack

import concourse.mybir as mybir
from concourse.masks import make_identity

F32 = mybir.dt.float32
BF16 = mybir.dt.bfloat16
U32 = mybir.dt.uint32
I32 = mybir.dt.int32
U8 = mybir.dt.uint8
FP8X4 = mybir.dt.float8_e4m3fn_x4
ALU = mybir.AluOpType
ACT = mybir.ActivationFunctionType

B, S, E, H, G, D = 4, 1024, 1024, 4, 2, 128
P = 128
PACK = 4
K_PASS = P * PACK
Q_TILES = S // P
BLOCKS = K_PASS // P
E_PASSES = E // K_PASS
KEY_PASSES = S // K_PASS
HEADS_PER_GROUP = H // G
SCALE = 1.0 / math.sqrt(D)
MASKED = -(2.0**100)
HALF = P // 2

FLOPS = 2 * B * G * S * E * D + 2 * 2 * B * H * D * (K_PASS * K_PASS + K_PASS * S)

MEMORY = (3, 2, 1, 0, 4, 5, 6, 7)
X_RUNS = (
    tuple((P * MEMORY[m], slice(32 * m, 32 * (m + 1)), slice(0, 4)) for m in range(4)),
    ((512, slice(0, 128), slice(0, 2)), (512, slice(0, 128), slice(2, 4))),
)
UNITS = (
    (2, ((7, 0, 8, 0),)),
    (2, ((6, 0, 7, 0), (0, 7, 8, 4))),
    (2, ((5, 0, 6, 0), (1, 6, 8, 4))),
    (2, ((4, 0, 5, 0), (2, 5, 8, 4))),
    (1, ((3, 0, 4, 0),)),
)
PAIRS = 3
FIRST_ORDER = (4, 0, 1, 2, 3)
ORDER_OF_UNITS = (FIRST_ORDER,) + ((0, 1, 2, 3, 4),) * (B - 1)
Q_ORDER = tuple(tuple(part[0] for u in order for part in UNITS[u][1]) for order in ORDER_OF_UNITS)
STEPS_PER_BATCH = len(UNITS) * H
MARGIN = 3
ON_S = ((3, 3, 0), (3, 3, 1))
W_ROUND = 6
ORDER = [("s",0),("v",0),("t",4),("n",0),("r",0),("e",2),("c",4),("q",6),("p",0)]
PLAN = [("x0",3),("x1",4),("x2",5),("x3",6),("x4",7),("x5",8),("x6",9),("x7",10),("v0",8),("v1",9),("v2",12),("v3",13),("q2",5),("q3",9),("K0",14),("Q0",16),("K1",17),("Q1",19)]
PLAN0 = [("kA1",0),("qB",1),("kB0",2),("kB1",3),("x0",5),("x1",6),("x2",7),("x3",8),("x4",9),("x5",10),("x6",11),("x7",12),("v0",10),("v1",11),("v2",14),("v3",15),("q1",5),("q2",8),("q3",12),("K0",15),("Q0",17),("K1",18),("Q1",19)]
NX = 4


def tile_multiheadattention_pa_t_kernel(tc, q, kg, x, Wv, bv, out):
    nc = tc.nc
    with ExitStack() as ctx:
        consts = ctx.enter_context(tc.tile_pool(name="consts", bufs=1))
        batch = ctx.enter_context(tc.tile_pool(name="batch", bufs=2))
        work = ctx.enter_context(tc.tile_pool(name="work", bufs=6))
        prep = ctx.enter_context(tc.tile_pool(name="prep", bufs=2))
        ring = ctx.enter_context(tc.tile_pool(name="ring", bufs=8))
        wide = ctx.enter_context(tc.tile_pool(name="wide", bufs=4))
        rows = ctx.enter_context(tc.tile_pool(name="rows", bufs=5))
        small = ctx.enter_context(tc.tile_pool(name="small", bufs=24))
        psum = ctx.enter_context(tc.psum_pool(name="psum", bufs=8))

        tiles = [{} for b in range(B)]

        def tiles_of(b):
            t = tiles[b]
            t["k"] = batch.tile([P, G * Q_TILES * D], BF16, name="k_sb")
            t["q"] = batch.tile([P, H * Q_TILES * D], BF16, name="q_sb")
            t["kT"] = batch.tile([P, G * S], BF16, name="kT")
            t["qT"] = batch.tile([P, H * S], BF16, name="qT")
            t["x"] = batch.tile([P, (S // P) * E], BF16, name="x_sb")
            t["x_codes"] = batch.tile([P, (S // P) * E_PASSES * P], U32, name="x_codes", align_bytes=64)
            t["x_scales"] = batch.tile([P, (S // P) * E_PASSES * P], U8, name="x_scales", align_bytes=64)
            t["v_codes"] = batch.tile([P, KEY_PASSES * G * D], U32, name="v_codes", align_bytes=64)
            t["v_scales"] = v_scales[b % 2]

        def load_k(b, g, i0, i1):
            first = g * Q_TILES
            nc.sync.dma_start(
                out=tiles[b]["k"][:, (first + i0) * D : (first + i1) * D].rearrange("p (i d) -> p i d", d=D),
                in_=kg[b, g, i0 * P : i1 * P, :].rearrange("(i p) d -> p i d", p=P),
            )

        def load_q(b, place):
            width = H * D
            i = Q_ORDER[b][place]
            nc.sync.dma_start(
                out=tiles[b]["q"][:, place * width : (place + 1) * width].rearrange("p (h d) -> p h d", d=D),
                in_=q[b, :, i * P : (i + 1) * P, :].rearrange("h p d -> p h d"),
            )

        def load_x(b, c, n):
            width = PACK * E
            first, parts, slots = X_RUNS[c][n]
            count = parts.stop - parts.start
            nc.sync.dma_start(
                out=tiles[b]["x"][parts, c * width + slots.start * E : c * width + slots.stop * E].rearrange(
                    "p (t k) -> p t k", k=E
                ),
                in_=x[b, first : first + PACK * count, :].rearrange("(p t) k -> p t k", t=PACK)[:, slots, :],
            )

        LOADS = [(load_k, 0, 0, 8), (load_q, 0), (load_q, 1), (load_k, 1, 0, 8), (load_q, 2), (load_q, 3)]
        FIRST_LOADS = [(load_k, 0, 0, 4), (load_q, 0), (load_k, 1, 0, 4), (load_q, 1), (load_k, 0, 4, 8), (load_k, 1, 4, 8)]
        REST = [(load_x, 0, n) for n in range(len(X_RUNS[0]))]
        REST_X1 = [(load_x, 1, n) for n in range(len(X_RUNS[1]))]
        LOADS += REST + [(load_q, 4), (load_q, 5)] + REST_X1 + [(load_q, 6), (load_q, 7)]
        FIRST_LOADS += REST[:NX] + [(load_q, 2), (load_q, 3)] + REST[NX:] + [(lambda b: load_w(b),)] + [(load_q, 4), (load_q, 5)] + REST_X1 + [(load_q, 6), (load_q, 7)]


        ident_f = consts.tile([P, P], F32, name="ident_f")
        make_identity(nc, ident_f[:])
        ident_bf = consts.tile([P, P], BF16, name="ident_bf")
        make_identity(nc, ident_bf[:])
        mask_f = consts.tile([P, P], F32, name="mask_f")
        nc.gpsimd.memset(mask_f[:], 0.0)
        nc.gpsimd.affine_select(
            out=mask_f[:],
            in_=mask_f[:],
            pattern=[[-1, P]],
            compare_op=ALU.is_ge,
            fill=MASKED,
            base=0,
            channel_multiplier=1,
        )
        mask_bf = consts.tile([P, P], BF16, name="mask_bf")
        nc.vector.tensor_copy(out=mask_bf[:], in_=mask_f[:])

        warm_ps = psum.tile([P, K_PASS], F32, name="warm_ps", tag="bank")
        for n in range(10):
            nc.tensor.matmul(warm_ps[:, :P], lhsT=ident_bf[:], rhs=ident_bf[:], start=True, stop=True)

        v_scales = []
        for n in range(2):
            scales = consts.tile([P, KEY_PASSES * G * D], U8, name="v_scales%d" % n, align_bytes=64)
            nc.gpsimd.memset(scales[:].bitcast(U32), 0)
            v_scales.append(scales)
        part_codes, part_scales = {}, {}
        for u in range(1, PAIRS + 1):
            codes_u = consts.tile([P, KEY_PASSES * G * D], U32, name="part_codes%d" % u, align_bytes=64)
            scales_u = consts.tile([P, KEY_PASSES * G * D], U8, name="part_scales%d" % u, align_bytes=64)
            nc.gpsimd.memset(codes_u[:], 0)
            nc.gpsimd.memset(scales_u[:].bitcast(U32), 0)
            part_codes[u], part_scales[u] = codes_u, scales_u

        w_wide = wide.tile([P, 2 * E_PASSES * G * D * PACK], BF16, name="w_wide", tag="e_grp", align_bytes=64)
        w_raw = w_wide[:, : E_PASSES * G * D * PACK].rearrange("p (a k) -> p a k", k=2 * D)
        w_grp = w_wide[:, E_PASSES * G * D * PACK :].rearrange("p (a d t) -> p a d t", d=D, t=PACK)
        w_codes = consts.tile([P, E_PASSES * G * D], U32, name="w_codes", align_bytes=64)
        w_scales = consts.tile([P, E_PASSES * G * D], U8, name="w_scales", align_bytes=64)
        bv_row = consts.tile([P, G * D], BF16, name="bv_row")
        nc.gpsimd.memset(bv_row[:], 0.0)
        ones = consts.tile([P, P], BF16, name="ones")
        nc.gpsimd.memset(ones[:], 1.0)
        bv_all = consts.tile([P, G * D], BF16, name="bv_all")

        def load_w(b):
            nc.sync.dma_start(out=w_raw, in_=Wv.rearrange("g (a p e) d -> p (g a) (e d)", p=P, e=2))
            nc.sync.dma_start(out=bv_row[0:1, :], in_=bv.rearrange("(o g) d -> o (g d)", o=1))

        def spread_bv():
            spread = psum.tile([P, K_PASS], F32, name="spread", tag="bank")
            nc.tensor.matmul(spread[:, : G * D], lhsT=ones[:], rhs=bv_row[:], start=True, stop=True)
            nc.scalar.copy(out=bv_all[:], in_=spread[:, : G * D])

        def group_w():
            for c in range(E_PASSES):
                for g in range(G):
                    first = (g * E_PASSES + c) * 2
                    nc.vector.tensor_copy(
                        out=w_grp[:, c * G + g, :, :].rearrange("p d (u e) -> p d u e", u=2),
                        in_=w_raw[:, first : first + 2, :].rearrange("p u (e d) -> p d u e", e=2),
                    )

        def quantise_w():
            nc.vector.quantize_mx(
                out=w_codes[:].bitcast(FP8X4),
                scales=w_scales[:],
                in_=w_wide[:, E_PASSES * G * D * PACK :],
            )

        warm = consts.tile([P, 1], F32, name="warm")
        nc.vector.memset(warm[:], 0.0)
        nc.scalar.activation(out=warm[:], in_=warm[:], func=ACT.Exp)

        tiles_of(0)
        for what, *where in FIRST_LOADS:
            what(0, *where)

        def x_piece(t, j):
            held = {}
            x_words = t["x"][:].bitcast(F32)
            words = E // 2
            width = E_PASSES * K_PASS

            def on_tensor():
                held["ps"] = psum.tile([P, E_PASSES * 2, P], F32, name="xt_ps", tag="bank")
                for cu in range(E_PASSES * 2):
                    nc.tensor.transpose(
                        held["ps"][:, cu, :],
                        x_words[:, j * words + cu * P : j * words + (cu + 1) * P],
                        ident_f[:],
                    )

            def out_of_psum():
                if j % 2 == 0:
                    t["x_grp"] = prep.tile([P, 2 * width], BF16, name="x_grp", align_bytes=64)
                nc.scalar.copy(
                    out=t["x_grp"][:]
                    .bitcast(F32)[:, (j % 2) * width // 2 : (j % 2 + 1) * width // 2]
                    .rearrange("p (c s u) -> p c s u", c=E_PASSES, u=2),
                    in_=held["ps"][:].rearrange("p (c u) s -> p c s u", u=2),
                )
                held["grp"] = t["x_grp"]

            def quantise():
                cols = slice((j - 1) * E_PASSES * P, (j + 1) * E_PASSES * P)
                nc.vector.quantize_mx(
                    out=t["x_codes"][:, cols].bitcast(FP8X4),
                    scales=t["x_scales"][:, cols],
                    in_=held["grp"][:],
                )

            return on_tensor, out_of_psum, quantise if j % 2 == 1 else None, None

        def v_piece(t, kp, g):
            held = {}

            def on_tensor():
                held["ps"] = psum.tile([P, PACK, D], F32, name="v_ps", tag="bank")
                for tt in range(PACK):
                    j = kp * PACK + tt
                    for c in range(E_PASSES):
                        x_cols = slice((j * E_PASSES + c) * P, (j * E_PASSES + c + 1) * P)
                        w_cols = slice((c * G + g) * D, (c * G + g + 1) * D)
                        nc.tensor.matmul_mx(
                            out=held["ps"][:, tt, :],
                            lhsT=t["x_codes"][:, x_cols].bitcast(FP8X4),
                            lhsT_scale=t["x_scales"][:, x_cols],
                            rhs=w_codes[:, w_cols].bitcast(FP8X4),
                            rhs_scale=w_scales[:, w_cols],
                            start=(c == 0),
                            stop=(c == E_PASSES - 1),
                        )

            def out_of_psum():
                if g == 0:
                    t["v_grp"] = prep.tile([P, G * D * PACK], BF16, name="v_grp", align_bytes=64)
                nc.vector.tensor_tensor(
                    out=t["v_grp"][:, g * D * PACK : (g + 1) * D * PACK].rearrange("p (d t) -> p d t", t=PACK),
                    in0=held["ps"][:].rearrange("p t d -> p d t"),
                    in1=bv_all[:, g * D : (g + 1) * D].unsqueeze(2).to_broadcast([P, D, PACK]),
                    op=ALU.add,
                )
                held["grp"] = t["v_grp"]

            cols = slice(kp * G * D, (kp + 1) * G * D)

            def quantise():
                nc.vector.quantize_mx(
                    out=t["v_codes"][:, cols].bitcast(FP8X4),
                    scales=t["v_scales"][:, cols],
                    in_=held["grp"][:],
                )

            def restrict(u):
                bound = 32 * (UNITS[u][1][0][2] - BLOCKS)
                rows = slice(bound, P) if kp == 0 else slice(0, bound)
                nc.sync.dma_start(
                    out=part_codes[u][rows, cols].bitcast(I32), in_=t["v_codes"][rows, cols].bitcast(I32)
                )
                nc.sync.dma_start(
                    out=part_scales[u][rows, cols].bitcast(I32), in_=t["v_scales"][rows, cols].bitcast(I32)
                )

            if g < G - 1:
                return on_tensor, out_of_psum, None, None
            return on_tensor, out_of_psum, quantise, restrict

        def head_piece(rows, transposed, n, places, i0=0, i1=Q_TILES):
            held = {}

            def on_tensor():
                held["ps"] = psum.tile([P, S], BF16, name="hT_ps", tag="bank")
                for i in range(i0, i1):
                    nc.tensor.transpose(
                        held["ps"][:, places[i] * P : (places[i] + 1) * P],
                        rows[:, (n * Q_TILES + i) * D : (n * Q_TILES + i + 1) * D],
                        ident_bf[:],
                    )

            def out_of_psum():
                nc.scalar.copy(
                    out=transposed[:, n * S + i0 * P : n * S + i1 * P].bitcast(F32),
                    in_=held["ps"][:, i0 * P : i1 * P].bitcast(F32),
                )

            return on_tensor, out_of_psum, None, None

        def k_piece(t, g, *blocks):
            return head_piece(t["k"], t["kT"], g, [MEMORY.index(i) for i in range(Q_TILES)], *blocks)

        def q_piece(t, n, *rows):
            return head_piece(t["q"], t["qT"], n, range(Q_TILES), *rows)

        pieces_of_round = {}

        def run_pieces(k):
            for piece in pieces_of_round.get(k, []):
                piece[0]()
                piece[1]()
            for piece in pieces_of_round.get(k - 1, []):
                if piece[2] is not None:
                    piece[2]()
            for u in range(1, PAIRS + 1):
                for piece in pieces_of_round.get(k - 2 - u, []):
                    if piece[3] is not None:
                        piece[3](u)

        steps = [(b, u, h) for b in range(B) for u in ORDER_OF_UNITS[b] for h in range(H)]
        state = [{} for step in steps]
        shared = {}

        def scores(n):
            b, u, h = steps[n]
            passes, parts = UNITS[u]
            g = h // HEADS_PER_GROUP
            kT = tiles[b]["kT"]
            state[n]["s"] = []
            for c in range(passes):
                s_ps = psum.tile([P, K_PASS], F32, name="s_ps", tag="bank")
                state[n]["s"].append(s_ps)
                for i, m0, m1, shift in parts:
                    place = Q_ORDER[b].index(i) * H + h
                    q_cols = tiles[b]["qT"][:, place * P : (place + 1) * P]
                    lo, hi = max(m0, c * BLOCKS), min(m1, (c + 1) * BLOCKS)
                    diagonal = MEMORY.index(i) + shift
                    if lo <= diagonal < hi:
                        runs = ((lo, diagonal), (diagonal, diagonal + 1), (diagonal + 1, hi))
                    else:
                        runs = ((lo, hi),)
                    for first, last in runs:
                        if first >= last:
                            continue
                        cols = slice((first - c * BLOCKS) * P, (last - c * BLOCKS) * P)
                        keys = slice(g * S + (first - shift) * P, g * S + (last - shift) * P)
                        masked = first == diagonal
                        nc.tensor.matmul(s_ps[:, cols], lhsT=q_cols, rhs=kT[:, keys], start=True, stop=not masked)
                        if masked:
                            nc.tensor.matmul(s_ps[:, cols], lhsT=ident_bf[:], rhs=mask_bf[:], start=False, stop=True)

        def rowmax(n):
            b, u, h = steps[n]
            passes, parts = UNITS[u]
            minus_s = ring.tile([P, 2, passes * K_PASS // 2], F32, name="minus_s")
            state[n]["minus_s"] = minus_s
            state[n]["shift"] = []
            for i, m0, m1, shift in parts:
                ranges = []
                for c in range(passes):
                    lo, hi = max(m0, c * BLOCKS), min(m1, (c + 1) * BLOCKS)
                    if lo < hi:
                        ranges.append((c, lo, hi))
                lowest = small.tile([P, 2], F32, name="lowest")
                for column, (c, lo, hi) in enumerate(ranges):
                    nc.vector.tensor_scalar(
                        out=minus_s[:, :, lo * HALF : hi * HALF].rearrange("p w (m e) -> p w m e", e=2),
                        in0=state[n]["s"][c][:, (lo - c * BLOCKS) * P : (hi - c * BLOCKS) * P].rearrange(
                            "p (m w e) -> p w m e", w=2, e=2
                        ),
                        scalar1=-SCALE,
                        scalar2=None,
                        op0=ALU.mult,
                        op1=ALU.min,
                        accum_out=lowest[:, column : column + 1],
                    )
                if len(ranges) == 1:
                    state[n]["shift"].append(lowest[:, 0:1])
                else:
                    joined = small.tile([P, 1], F32, name="joined")
                    nc.gpsimd.tensor_scalar(
                        out=joined[:], in0=lowest[:, 0:1], scalar1=lowest[:, 1:2], scalar2=None, op0=ALU.min
                    )
                    state[n]["shift"].append(joined[:])

        def exponential(n):
            b, u, h = steps[n]
            passes, parts = UNITS[u]
            if h == 0:
                shared[(b, u)] = {"sums": small.tile([P, len(parts) * H], F32, name="sums")}
            e_row = rows.tile([P, 2, passes * K_PASS // 2], BF16, name="e_row")
            state[n]["e_row"] = e_row
            for part, (i, m0, m1, shift) in enumerate(parts):
                nc.scalar.activation(
                    out=e_row[:, :, m0 * HALF : m1 * HALF],
                    in_=state[n]["minus_s"][:, :, m0 * HALF : m1 * HALF],
                    func=ACT.Exp,
                    bias=state[n]["shift"][part],
                    scale=-1.0,
                    accum_out=shared[(b, u)]["sums"][:, part * H + h : part * H + h + 1],
                )

        def transposes(n):
            b, u, h = steps[n]
            passes, parts = UNITS[u]
            if passes == 2 or h % 2 == 0:
                et_ps = psum.tile([P, 2 * 2, P], F32, name="et_ps", tag="bank")
            else:
                et_ps = state[n - 1]["et_ps"]
            state[n]["et_ps"] = et_ps
            e_words = state[n]["e_row"][:].rearrange("p w k -> p (w k)").bitcast(F32)
            for c in range(passes):
                for w in range(2):
                    slot = c * 2 + w if passes == 2 else (h % 2) * 2 + w
                    first = (w * passes + c) * P
                    nc.tensor.transpose(et_ps[:, slot, :], e_words[:, first : first + P], ident_f[:])

        def out_of_psum(n):
            b, u, h = steps[n]
            passes, parts = UNITS[u]
            if h == 0:
                shared[(b, u)]["e_grp"] = wide.tile([P, H * passes * K_PASS], BF16, name="e_grp", tag="e_grp", align_bytes=64)
            if passes == 1 and h % 2 == 0:
                return
            first = (h * passes - (1 if passes == 1 else 0)) * K_PASS // 2
            nc.scalar.copy(
                out=shared[(b, u)]["e_grp"][:]
                .bitcast(F32)[:, first : first + K_PASS]
                .rearrange("p (c s w) -> p c s w", c=2, w=2),
                in_=state[n]["et_ps"][:].rearrange("p (c w) s -> p c s w", w=2),
            )

        def quantise(b, u, heads):
            passes, parts = UNITS[u]
            if heads[0] == 0:
                shared[(b, u)]["e_codes"] = wide.tile([P, H * passes * P], U32, name="e_codes", align_bytes=64)
                shared[(b, u)]["e_scales"] = wide.tile([P, H * passes * P], U8, name="e_scales", align_bytes=64)
                shared[(b, u)]["inverse"] = small.tile([P, len(parts) * H], F32, name="inverse")
                shared[(b, u)]["o_ps"] = {}
            cols = slice(heads[0] * passes * P, (heads[-1] + 1) * passes * P)
            nc.vector.quantize_mx(
                out=shared[(b, u)]["e_codes"][:, cols].bitcast(FP8X4),
                scales=shared[(b, u)]["e_scales"][:, cols],
                in_=shared[(b, u)]["e_grp"][:, cols.start * PACK : cols.stop * PACK],
            )
            sums = slice(heads[0], heads[-1] + 1 + (len(parts) - 1) * H)
            nc.vector.reciprocal(
                out=shared[(b, u)]["inverse"][:, sums], in_=shared[(b, u)]["sums"][:, sums]
            )

        def weighted_values(b, u, part, heads):
            passes, parts = UNITS[u]
            t = tiles[b]
            o_ps = psum.tile([P, H * D], F32, name="o_ps", tag="bank")
            shared[(b, u)]["o_ps"][(part, heads)] = o_ps
            full = (t["v_codes"], t["v_scales"])
            half = (part_codes.get(u), part_scales.get(u))
            if part == 1:
                uses = ((1, half, 0),)
            elif len(parts) == 2:
                uses = ((0, full, 0), (1, half, 1))
            else:
                uses = tuple((c, full, c) for c in range(passes))
            for h in heads:
                g = h // HEADS_PER_GROUP
                for place, (c, (codes, scales), kp) in enumerate(uses):
                    e_cols = slice((h * passes + c) * P, (h * passes + c + 1) * P)
                    v_cols = slice((kp * G + g) * D, (kp * G + g + 1) * D)
                    nc.tensor.matmul_mx(
                        out=o_ps[:, h * D : (h + 1) * D],
                        lhsT=shared[(b, u)]["e_codes"][:, e_cols].bitcast(FP8X4),
                        lhsT_scale=shared[(b, u)]["e_scales"][:, e_cols],
                        rhs=codes[:, v_cols].bitcast(FP8X4),
                        rhs_scale=scales[:, v_cols],
                        start=(place == 0),
                        stop=(place == len(uses) - 1),
                    )

        def on_scalar(b, u, part):
            return (b, u, part) in ON_S

        def normalise_and_store(b, u, part, heads):
            passes, parts = UNITS[u]
            i = parts[part][0]
            o_sb = work.tile([P, H * D], F32, name="o_sb", tag="o")
            count = len(heads)
            cols = slice(heads[0] * D, (heads[-1] + 1) * D)
            sums = slice(part * H + heads[0], part * H + heads[-1] + 1)
            if on_scalar(b, u, part):
                for h in heads:
                    nc.scalar.activation(
                        out=o_sb[:, h * D : (h + 1) * D],
                        in_=shared[(b, u)]["o_ps"][(part, heads)][:, h * D : (h + 1) * D],
                        func=ACT.Copy,
                        scale=shared[(b, u)]["inverse"][:, part * H + h : part * H + h + 1],
                    )
            else:
                nc.vector.tensor_tensor(
                    out=o_sb[:, cols].rearrange("p (h d) -> p h d", h=count),
                    in0=shared[(b, u)]["o_ps"][(part, heads)][:, cols].rearrange("p (h d) -> p h d", h=count),
                    in1=shared[(b, u)]["inverse"][:, sums].unsqueeze(2).to_broadcast([P, count, D]),
                    op=ALU.mult,
                )
            nc.sync.dma_start(out=out[b, i * P : (i + 1) * P, cols], in_=o_sb[:, cols])

        def at(stage, n):
            if 0 <= n < len(steps):
                stage(n)

        ctx.enter_context(tc.manual_schedule())
        for piece in (k_piece(tiles[0], 0, 0, 4), q_piece(tiles[0], 0, 0, 4)):
            piece[0]()
            piece[1]()

        waiting = []
        done = {}
        lags = dict(ORDER)
        k = -1
        while k < len(steps) + lags["q"] or waiting or done:
            k += 1
            b_now = k // STEPS_PER_BATCH
            if k % STEPS_PER_BATCH == 0 and b_now < B:
                t = tiles[b_now]
                own = {"x%d" % j: x_piece(t, j) for j in range(S // P)}
                own.update({"v%d" % (kp * G + g): v_piece(t, kp, g) for kp in range(KEY_PASSES) for g in range(G)})
                own.update({"q%d" % n: q_piece(t, n) for n in range(1 if b_now == 0 else 2, 4)})
                if b_now == 0:
                    own.update({"qB": q_piece(t, 0, 4, 8), "kA1": k_piece(t, 1, 0, 4), "kB0": k_piece(t, 0, 4, 8), "kB1": k_piece(t, 1, 4, 8)})
                if b_now + 1 < B:
                    tiles_of(b_now + 1)
                    own.update({"K0": k_piece(tiles[b_now + 1], 0), "K1": k_piece(tiles[b_now + 1], 1), "Q0": q_piece(tiles[b_now + 1], 0), "Q1": q_piece(tiles[b_now + 1], 1)})
                for name, rnd in PLAN0 if b_now == 0 else PLAN:
                    if name in own:
                        pieces_of_round.setdefault(k + rnd, []).append(own[name])
            if b_now + 1 < B and k % STEPS_PER_BATCH < len(LOADS):
                what, *where = LOADS[k % STEPS_PER_BATCH]
                what(b_now + 1, *where)
            if k == W_ROUND:
                group_w()
            if k == W_ROUND + 1:
                quantise_w()
                spread_bv()
            for stage, lag in ORDER:
                if stage == "s":
                    at(scores, k - lag)
                if stage == "r":
                    at(rowmax, k - lag)
                if stage == "e":
                    at(exponential, k - lag)
                if stage == "t":
                    at(transposes, k - lag)
                if stage == "c":
                    at(out_of_psum, k - lag)
                if stage == "q":
                    n = k - lag
                    if 0 <= n < len(steps):
                        b, u, h = steps[n]
                        count = 2 if (b, u) == (B - 1, len(UNITS) - 1) else H
                        if h % count == count - 1:
                            heads = tuple(range(h + 1 - count, h + 1))
                            quantise(b, u, heads)
                            for part in range(len(UNITS[u][1])):
                                plan = dict(PLAN0 if b == 0 else PLAN)
                                made = plan["v3"] if UNITS[u][0] == 2 else plan["v1"]
                                vg = b * STEPS_PER_BATCH + made + (4 + u if len(UNITS[u][1]) == 2 else 2)
                                waiting.append((max(k + MARGIN, vg), (b, u, part, heads)))
                if stage == "p":
                    run_pieces(k)
                if stage == "v" and (k % 2 == 0 or k >= len(steps)) and waiting and waiting[0][0] <= k:
                    done[k + 1] = waiting.pop(0)[1]
                    weighted_values(*done[k + 1])
                if stage == "n" and k in done and not on_scalar(*done[k][:3]):
                    normalise_and_store(*done.pop(k))
                if stage == "p" and k in done:
                    normalise_and_store(*done.pop(k))
